import numpy as np
import ml_dtypes


def mxq(x, axis, fmt="e4m3"):
    dtype, down = {"e4m3": (ml_dtypes.float8_e4m3fn, 7), "e5m2": (ml_dtypes.float8_e5m2, 14)}[fmt]
    v = np.moveaxis(np.asarray(x, np.float32).astype(ml_dtypes.bfloat16).astype(np.float64), axis, -1)
    blocks = v.reshape(v.shape[:-1] + (-1, 32))
    amax = np.abs(blocks).max(-1, keepdims=True)
    byte = np.maximum(np.where(amax > 0, np.frexp(amax)[1] - 1 + 127, 0) - down, 1)
    scale = np.exp2(byte - 127.0)
    codes = (blocks / scale).astype(np.float32).astype(dtype).astype(np.float64)
    return np.moveaxis((codes * scale).reshape(v.shape), -1, axis)


WIDE = False


def mx_kscale(k):
    if not WIDE:
        return np.ones(k)
    levels = np.array([10, -10, 5, -5, 0])
    if k % 512:
        return np.exp2(np.random.permutation(np.resize(levels, k // 32))).repeat(32)
    a = np.empty((k // 512, 16))
    for p in range(k // 512):
        a[p, :8] = np.random.permutation(np.resize(levels, 8))
        for g in range(8):
            far = levels[np.abs(levels - a[p, g]) >= 10]
            a[p, g + 8] = far[np.random.randint(len(far))]
    return np.exp2(a.ravel()).repeat(32)


BF16 = ml_dtypes.bfloat16


def bf(x):
    return np.asarray(x, np.float32).astype(BF16)


def f64(x):
    return np.asarray(x).astype(np.float64)


B, S, D, E, HD = 4, 1024, 512, 1024, 64
ROPE_BASE = 10000.0


def rope_tables():
    inv_freq = 1.0 / ROPE_BASE ** (np.arange(0, E, 2) / E)
    ang = np.repeat(np.arange(S)[:, None] * inv_freq[None, :], 2, axis=-1)
    return np.cos(ang), np.sin(ang)


def rotate_half(v):
    h = v.shape[-1] // 2
    return np.concatenate([-v[..., h:], v[..., :h]], axis=-1)


def setup_inputs():
    s = mx_kscale(D)
    return {"x": bf(np.random.standard_normal((B, S, D)) * s),
            "Wq": bf(np.random.standard_normal((D, E)) * 0.5 / np.sqrt(D) / s[:, None]),
            "bq": bf(np.random.standard_normal(E) * 0.1),
            "Wk": bf(np.random.standard_normal((D, E)) * 0.5 / np.sqrt(D) / s[:, None]),
            "bk": bf(np.random.standard_normal(E) * 0.1)}


def reference(x, Wq, bq, Wk, bk):
    xq = mxq(f64(x), 2, "e4m3")
    q = (xq @ mxq(f64(Wq), 0, "e4m3")) + f64(bq)
    k = (xq @ mxq(f64(Wk), 0, "e4m3")) + f64(bk)
    cos, sin = rope_tables()
    qr = q * cos + rotate_half(q) * sin
    kr = k * cos + rotate_half(k) * sin
    return qr, kr

@@ -1,0 +1,342 @@
+from contextlib import ExitStack
+
+import concourse.masks as masks
+import concourse.mybir as mybir
+
+F32 = mybir.dt.float32
+BF16 = mybir.dt.bfloat16
+U32 = mybir.dt.uint32
+U8 = mybir.dt.uint8
+FP8X4 = mybir.dt.float8_e4m3fn_x4
+ALU = mybir.AluOpType
+ACT = mybir.ActivationFunctionType
+
+P = 128
+PACK = 4
+BATCH, SEQ, D_IN, D_OUT = 4, 1024, 512, 1024
+ROPE_BASE = 10000.0
+PI = 3.141592653589793
+assert D_IN == P * PACK
+
+N_BLOCKS = SEQ // P
+TOKENS = BATCH * P
+N_FT = D_OUT // P
+HALF_FT = N_FT // 2
+PAIRS_PER_BLOCK = 2 * HALF_FT
+N_PAIRS = N_BLOCKS * PAIRS_PER_BLOCK
+N_TRIG = 2 * N_FT
+
+FREQ_STEP = ROPE_BASE ** (-2.0 / D_OUT)
+ROUND_MAGIC = 12582912.0
+
+FLOPS = 2 * BATCH * SEQ * D_IN * 2 * D_OUT
+
+
+def tile_ropemultiheadattention_pa_t_kernel(tc, x, Wq, bq, Wk, bk, out_0, out_1):
+    nc = tc.nc
+    outs = (out_0, out_1)
+    with ExitStack() as ctx:
+        ctx.enter_context(tc.manual_schedule())
+        const = ctx.enter_context(tc.tile_pool(name="const", bufs=1))
+        xq_pool = ctx.enter_context(tc.tile_pool(name="xq", bufs=2))
+        fold_pool = ctx.enter_context(tc.tile_pool(name="fold", bufs=1))
+        trig_pool = ctx.enter_context(tc.tile_pool(name="trig", bufs=2))
+        prod_pool = ctx.enter_context(tc.tile_pool(name="prod", bufs=3))
+        stage_pool = ctx.enter_context(tc.tile_pool(name="stage", bufs=3))
+        mx_psum = ctx.enter_context(tc.psum_pool(name="mx_psum", bufs=4))
+        sum_psum = ctx.enter_context(tc.psum_pool(name="sum_psum", bufs=3))
+        xt_psum = ctx.enter_context(tc.psum_pool(name="xt_psum", bufs=1))
+
+        xin = const.tile([P, N_BLOCKS, BATCH, D_IN], BF16, name="xin")
+
+        def load_x(t):
+            nc.sync.dma_start(
+                out=xin[:, t, :, :], in_=x[:, t * P : (t + 1) * P, :].rearrange("b p k -> p b k")
+            )
+
+        def load_weight(w, label):
+            raw = const.tile([P, PACK, D_OUT], BF16, name="raw_" + label)
+            nc.sync.dma_start(out=raw[:], in_=w.rearrange("(q t) c -> q t c", t=PACK))
+            return raw
+
+        bias_rows = const.tile([P, P], BF16, name="bias_rows")
+        nc.vector.memset(bias_rows[:], 0.0)
+        load_x(0)
+        raw = [load_weight(Wq, "q")]
+        nc.sync.dma_start(out=bias_rows[0:N_FT, :], in_=bq.rearrange("(r c) -> r c", c=P))
+        nc.sync.dma_start(out=bias_rows[N_FT : 2 * N_FT, :], in_=bk.rearrange("(r c) -> r c", c=P))
+        raw.append(load_weight(Wk, "k"))
+        for t in range(1, N_BLOCKS):
+            load_x(t)
+
+        ident = const.tile([P, P], F32, name="ident")
+        masks.make_identity(nc, ident[:])
+
+        pos = const.tile([P, P], F32, name="pos")
+        nc.vector.memset(pos[:, 0:1], 0.0)
+        w = 1
+        while w < P:
+            nc.vector.tensor_scalar_add(out=pos[:, w : 2 * w], in0=pos[:, 0:w], scalar1=float(w))
+            w *= 2
+
+        step_row = const.tile([P, P], F32, name="step_row")
+        nc.vector.memset(step_row[:, 0:2], 1.0)
+        w = 2
+        while w < P:
+            nc.vector.tensor_scalar_mul(
+                out=step_row[:, w : 2 * w], in0=step_row[:, 0:w], scalar1=FREQ_STEP ** (w // 2)
+            )
+            w *= 2
+
+        minus_half = const.tile([P, 1], F32, name="minus_half")
+        nc.vector.memset(minus_half[:], -0.5)
+        half_pi = const.tile([P, 1], F32, name="half_pi")
+        nc.vector.tensor_scalar_mul(out=half_pi[:], in0=minus_half[:], scalar1=-PI)
+        minus_half_pi = const.tile([P, 1], F32, name="minus_half_pi")
+        nc.vector.tensor_scalar_mul(out=minus_half_pi[:], in0=minus_half[:], scalar1=PI)
+        warm = const.tile([P, 1], F32, name="warm")
+        nc.scalar.activation(out=warm[:], in_=half_pi[:], func=ACT.Sin)
+
+        step_col = sum_psum.tile([P, P], F32, name="step_col", tag="sums")
+        nc.tensor.transpose(out=step_col[:], in_=step_row[:], identity=ident[:])
+        turns = const.tile([P, N_FT], F32, name="turns")
+        nc.vector.tensor_scalar_mul(
+            out=turns[:, 0:1], in0=step_col[:, 0:1], scalar1=1.0 / (2.0 * PI)
+        )
+        w = 1
+        while w < N_FT:
+            nc.vector.tensor_scalar_mul(
+                out=turns[:, w : 2 * w], in0=turns[:, 0:w], scalar1=FREQ_STEP ** (w * P // 2)
+            )
+            w *= 2
+
+        def nearest_whole_removed(out, value, scratch):
+            nc.vector.tensor_scalar(
+                out=scratch, in0=value, scalar1=ROUND_MAGIC, scalar2=ROUND_MAGIC,
+                op0=ALU.add, op1=ALU.subtract,
+            )
+            nc.vector.tensor_tensor(out=out, in0=value, in1=scratch, op=ALU.subtract)
+
+        table_shape = [P, N_FT, P]
+        angle0 = const.tile(table_shape, F32, name="angle0")
+        nc.vector.tensor_tensor(
+            out=angle0[:],
+            in0=pos[:].unsqueeze(1).to_broadcast(table_shape),
+            in1=turns[:].unsqueeze(2).to_broadcast(table_shape),
+            op=ALU.mult,
+        )
+        whole0 = const.tile(table_shape, F32, name="whole0")
+        frac0 = const.tile(table_shape, F32, name="frac0")
+        nearest_whole_removed(frac0[:], angle0[:], whole0[:])
+
+        block_shape = [P, N_BLOCKS, N_FT]
+        block_turns = const.tile([P, N_FT], F32, name="block_turns")
+        nc.vector.tensor_scalar_mul(out=block_turns[:], in0=turns[:], scalar1=float(P))
+        block_angle = const.tile(block_shape, F32, name="block_angle")
+        nc.vector.tensor_tensor(
+            out=block_angle[:],
+            in0=pos[:, 0:N_BLOCKS].unsqueeze(2).to_broadcast(block_shape),
+            in1=block_turns[:].unsqueeze(1).to_broadcast(block_shape),
+            op=ALU.mult,
+        )
+        block_whole = const.tile(block_shape, F32, name="block_whole")
+        shifts = const.tile([P, N_BLOCKS, N_TRIG], F32, name="shifts")
+        nearest_whole_removed(shifts[:, :, N_FT:N_TRIG], block_angle[:], block_whole[:])
+        nc.vector.tensor_scalar_add(out=shifts[:, :, 0:N_FT], in0=shifts[:, :, N_FT:N_TRIG], scalar1=-0.25)
+
+        def group_weight(z):
+            grouped = const.tile([P, D_OUT, PACK], BF16, name="w_grouped%d" % z, align_bytes=64)
+            nc.vector.tensor_copy(
+                out=grouped[:].rearrange("p (c i) t -> p c t i", i=4),
+                in_=raw[z][:].rearrange("p t (c i) -> p c t i", i=4),
+            )
+            return grouped
+
+        def quantise_weight(z, grouped):
+            codes = const.tile([P, D_OUT], U32, name="w_codes%d" % z, align_bytes=64)
+            scales = const.tile([P, D_OUT], U8, name="w_scales%d" % z, align_bytes=64)
+            nc.vector.quantize_mx(
+                out=codes[:].bitcast(FP8X4), scales=scales[:], in_=grouped[:].rearrange("p c t -> p (c t)")
+            )
+            return codes, scales
+
+        fold_of, trig_of, x_grouped_of, x_quantised_of = {}, {}, {}, {}
+
+        def first_fold(t, tables):
+            if t not in fold_of:
+                fold_of[t] = fold_pool.tile([P, N_TRIG, P], F32, name="fold", tag="fold")
+            for i in tables:
+                nc.scalar.activation(
+                    out=fold_of[t][:, i, :], in_=frac0[:, i % N_FT, :], func=ACT.Abs,
+                    bias=shifts[:, t, i : i + 1],
+                )
+
+        def second_fold(t, tables):
+            nc.scalar.activation(
+                out=fold_of[t][:, tables, :], in_=fold_of[t][:, tables, :], func=ACT.Abs,
+                bias=minus_half[:, 0:1],
+            )
+
+        def sines(t):
+            trig_of[t] = trig_pool.tile([P, N_TRIG, P], F32, name="trig", tag="trig")
+            nc.scalar.activation(
+                out=trig_of[t][:, 0:HALF_FT, :], in_=fold_of[t][:, 0:HALF_FT, :], func=ACT.Sin,
+                scale=-2.0 * PI, bias=half_pi[:, 0:1],
+            )
+            nc.scalar.activation(
+                out=trig_of[t][:, HALF_FT:N_FT, :], in_=fold_of[t][:, HALF_FT:N_FT, :], func=ACT.Sin,
+                scale=2.0 * PI, bias=minus_half_pi[:, 0:1],
+            )
+
+        def cosines(t):
+            nc.scalar.activation(
+                out=trig_of[t][:, N_FT:N_TRIG, :], in_=fold_of[t][:, N_FT:N_TRIG, :], func=ACT.Sin,
+                scale=2.0 * PI, bias=minus_half_pi[:, 0:1],
+            )
+
+        def turn_x(t, first):
+            if first == 0:
+                x_grouped_of[t] = xq_pool.tile([P, TOKENS, 2], F32, name="x_grouped", tag="x_grouped", align_bytes=64)
+            xt = xt_psum.tile([P, 2, 2, P], F32, name="xt", tag="xt")
+            for b in range(2):
+                words = xin[:, t, first + b, :].bitcast(F32)
+                for u in range(2):
+                    nc.tensor.transpose(out=xt[:, b, u, :], in_=words[:, u : 2 * P : 2], identity=ident[:])
+            copy = nc.vector.tensor_copy if t == 0 else nc.scalar.copy
+            copy(
+                out=x_grouped_of[t][:, first * P : (first + 2) * P, :].rearrange("w (b p) u -> w b p u", b=2),
+                in_=xt[:].rearrange("w b u p -> w b p u"),
+            )
+
+        def quantise_x(t):
+            codes = xq_pool.tile([P, TOKENS], U32, name="x_codes", tag="x_codes", align_bytes=64)
+            scales = xq_pool.tile([P, TOKENS], U8, name="x_scales", tag="x_scales", align_bytes=64)
+            nc.vector.quantize_mx(
+                out=codes[:].bitcast(FP8X4),
+                scales=scales[:],
+                in_=x_grouped_of[t][:].rearrange("w c u -> w (c u)").bitcast(BF16),
+            )
+            x_quantised_of[t] = (codes, scales)
+
+        def prepare(t, part):
+            if part < 2:
+                turn_x(t, 2 * part)
+                first_fold(t, range(HALF_FT * part, HALF_FT * (part + 1)))
+            elif part == 2:
+                quantise_x(t)
+                first_fold(t, range(N_FT, N_TRIG))
+            elif part == 3:
+                second_fold(t, slice(0, N_FT))
+            elif part == 4:
+                second_fold(t, slice(N_FT, N_TRIG))
+            elif part == 5:
+                sines(t)
+            elif part == 6:
+                cosines(t)
+
+        banks_of, products_of, stage_of = {}, {}, {}
+        by_sequence = [P, BATCH, P]
+
+        def where(k):
+            t, rest = divmod(k, PAIRS_PER_BLOCK)
+            z, f = divmod(rest, HALF_FT)
+            return t, z, f
+
+        def project(k):
+            t, z, f = where(k)
+            x_codes, x_scales = x_quantised_of[t]
+            w_codes, w_scales = weights[z]
+            banks = []
+            for h in range(2):
+                features = slice((f + h * HALF_FT) * P, (f + h * HALF_FT + 1) * P)
+                bank = mx_psum.tile([P, TOKENS], F32, name="bank", tag="bank")
+                nc.tensor.matmul_mx(
+                    out=bank[:],
+                    lhsT=w_codes[:, features].bitcast(FP8X4),
+                    lhsT_scale=w_scales[:, features],
+                    rhs=x_codes[:].bitcast(FP8X4),
+                    rhs_scale=x_scales[:],
+                    start=True,
+                    stop=True,
+                )
+                banks.append(bank)
+            banks_of[k] = banks
+
+        def product(out, bank, bias_col, table):
+            nc.vector.scalar_tensor_tensor(
+                out=out.rearrange("f (b p) -> f b p", b=BATCH),
+                in0=bank[:].rearrange("f (b p) -> f b p", b=BATCH),
+                scalar=bias_col,
+                in1=table.unsqueeze(1).to_broadcast(by_sequence),
+                op0=ALU.add,
+                op1=ALU.mult,
+            )
+
+        def rotate(k):
+            t, z, f = where(k)
+            trig = trig_of[t]
+            own = prod_pool.tile([P, 2, TOKENS], F32, name="own", tag="own")
+            other = prod_pool.tile([P, 2, TOKENS], F32, name="other", tag="other")
+            for h in range(2):
+                tile_here = f + h * HALF_FT
+                tile_there = f + (1 - h) * HALF_FT
+                bias_col = bias[:, z * N_FT + tile_here : z * N_FT + tile_here + 1]
+                product(own[:, h, :], banks_of[k][h], bias_col, trig[:, N_FT + tile_here, :])
+                product(other[:, 1 - h, :], banks_of[k][h], bias_col, trig[:, tile_there, :])
+            products_of[k] = (own, other)
+
+        def sum_and_turn(k):
+            t, z, f = where(k)
+            own, other = products_of[k]
+            if f == 0:
+                stage_of[(t, z)] = stage_pool.tile([P, BATCH, D_OUT], F32, name="stage", tag="stage")
+            stage = stage_of[(t, z)]
+            for first in range(0, BATCH, 2):
+                sums = sum_psum.tile([P, 2, 2, P], F32, name="sums", tag="sums")
+                for b in range(2):
+                    tokens = slice((first + b) * P, (first + b + 1) * P)
+                    for h in range(2):
+                        nc.tensor.matmul(
+                            out=sums[:, b, h, :], lhsT=own[:, h, tokens], rhs=ident[:],
+                            is_transpose=True, start=True, stop=False,
+                        )
+                        nc.tensor.matmul(
+                            out=sums[:, b, h, :], lhsT=other[:, h, tokens], rhs=ident[:],
+                            is_transpose=True, start=False, stop=True,
+                        )
+                nc.scalar.copy(
+                    out=stage[:, first : first + 2, :].rearrange("p b (h c) -> p b h c", h=2)[
+                        :, :, :, f * P : (f + 1) * P
+                    ],
+                    in_=sums[:],
+                )
+            if f == HALF_FT - 1:
+                for b in range(BATCH):
+                    nc.sync.dma_start(out=outs[z][b, t * P : (t + 1) * P, :], in_=stage[:, b, :])
+
+        prepare(0, 0)
+        prepare(0, 1)
+        grouped_q = group_weight(0)
+        prepare(0, 2)
+        weights = [quantise_weight(0, grouped_q)]
+        project(0)
+        for part in range(3, PAIRS_PER_BLOCK):
+            prepare(0, part)
+        bias_rows_f32 = const.tile([P, P], F32, name="bias_rows_f32")
+        nc.vector.tensor_copy(out=bias_rows_f32[:], in_=bias_rows[:])
+        bias_cols = sum_psum.tile([P, P], F32, name="bias_cols", tag="sums")
+        nc.tensor.transpose(out=bias_cols[:], in_=bias_rows_f32[:], identity=ident[:])
+        bias = const.tile([P, 2 * N_FT], F32, name="bias")
+        nc.vector.tensor_copy(out=bias[:], in_=bias_cols[:, 0 : 2 * N_FT])
+        weights.append(quantise_weight(1, group_weight(1)))
+
+        for k in range(N_PAIRS + 1):
+            if k + 1 < N_PAIRS:
+                project(k + 1)
+            if k < N_PAIRS:
+                rotate(k)
+            if k >= 1:
+                sum_and_turn(k - 1)
+            t, part = divmod(k, PAIRS_PER_BLOCK)
+            if t + 1 < N_BLOCKS:
+                prepare(t + 1, part)

@@ -20,11 +20,14 @@ assert D_IN == P * PACK
 
 N_BLOCKS = SEQ // P
 TOKENS = BATCH * P
-N_FT = D_OUT // P
-HALF_FT = N_FT // 2
-PAIRS_PER_BLOCK = 2 * HALF_FT
+HALVES = 2
+GROUPS = 2
+PARITIES = 2
+N_FREQ = HALVES * GROUPS
+UNITS = GROUPS * PARITIES
+PAIRS_PER_BLOCK = 2 * UNITS
 N_PAIRS = N_BLOCKS * PAIRS_PER_BLOCK
-N_TRIG = 2 * N_FT
+MINUS_SIN, SIN, COS, KINDS = 0, 1, 2, 4
 
 FREQ_STEP = ROPE_BASE ** (-2.0 / D_OUT)
 ROUND_MAGIC = 12582912.0
@@ -41,7 +44,7 @@ def tile_ropemultiheadattention_pa_t_kernel(tc, x, Wq, bq, Wk, bk, out_0, out_1)
         xq_pool = ctx.enter_context(tc.tile_pool(name="xq", bufs=2))
         fold_pool = ctx.enter_context(tc.tile_pool(name="fold", bufs=1))
         trig_pool = ctx.enter_context(tc.tile_pool(name="trig", bufs=2))
-        prod_pool = ctx.enter_context(tc.tile_pool(name="prod", bufs=3))
+        prod_pool = ctx.enter_context(tc.tile_pool(name="prod", bufs=5))
         stage_pool = ctx.enter_context(tc.tile_pool(name="stage", bufs=3))
         mx_psum = ctx.enter_context(tc.psum_pool(name="mx_psum", bufs=4))
         sum_psum = ctx.enter_context(tc.psum_pool(name="sum_psum", bufs=3))
@@ -49,9 +52,10 @@ def tile_ropemultiheadattention_pa_t_kernel(tc, x, Wq, bq, Wk, bk, out_0, out_1)
 
         xin = const.tile([P, N_BLOCKS, BATCH, D_IN], BF16, name="xin")
 
-        def load_x(t):
+        def load_x(t, first, count):
             nc.sync.dma_start(
-                out=xin[:, t, :, :], in_=x[:, t * P : (t + 1) * P, :].rearrange("b p k -> p b k")
+                out=xin[:, t, first : first + count, :],
+                in_=x[first : first + count, t * P : (t + 1) * P, :].rearrange("b p k -> p b k"),
             )
 
         def load_weight(w, label):
@@ -59,65 +63,60 @@ def tile_ropemultiheadattention_pa_t_kernel(tc, x, Wq, bq, Wk, bk, out_0, out_1)
             nc.sync.dma_start(out=raw[:], in_=w.rearrange("(q t) c -> q t c", t=PACK))
             return raw
 
-        bias_rows = const.tile([P, P], BF16, name="bias_rows")
-        nc.vector.memset(bias_rows[:], 0.0)
-        load_x(0)
+        bias_rows = const.tile([P, PARITIES * P], BF16, name="bias_rows")
+        nc.gpsimd.memset(bias_rows[:], 0.0)
+        load_x(0, 0, 2)
+        load_x(0, 2, 2)
+        nc.sync.dma_start(out=bias_rows[0:N_FREQ, :], in_=bq.rearrange("(r c) -> r c", r=N_FREQ))
+        nc.sync.dma_start(out=bias_rows[N_FREQ : 2 * N_FREQ, :], in_=bk.rearrange("(r c) -> r c", r=N_FREQ))
         raw = [load_weight(Wq, "q")]
-        nc.sync.dma_start(out=bias_rows[0:N_FT, :], in_=bq.rearrange("(r c) -> r c", c=P))
-        nc.sync.dma_start(out=bias_rows[N_FT : 2 * N_FT, :], in_=bk.rearrange("(r c) -> r c", c=P))
         raw.append(load_weight(Wk, "k"))
         for t in range(1, N_BLOCKS):
-            load_x(t)
+            load_x(t, 0, BATCH)
 
         ident = const.tile([P, P], F32, name="ident")
         masks.make_identity(nc, ident[:])
-
         pos = const.tile([P, P], F32, name="pos")
-        nc.vector.memset(pos[:, 0:1], 0.0)
-        w = 1
-        while w < P:
-            nc.vector.tensor_scalar_add(out=pos[:, w : 2 * w], in0=pos[:, 0:w], scalar1=float(w))
-            w *= 2
-
-        step_row = const.tile([P, P], F32, name="step_row")
-        nc.vector.memset(step_row[:, 0:2], 1.0)
-        w = 2
-        while w < P:
-            nc.vector.tensor_scalar_mul(
-                out=step_row[:, w : 2 * w], in0=step_row[:, 0:w], scalar1=FREQ_STEP ** (w // 2)
-            )
-            w *= 2
+        nc.gpsimd.iota(
+            pos[:], pattern=[[1, P]], base=0, channel_multiplier=0, allow_small_or_imprecise_dtypes=True
+        )
 
         minus_half = const.tile([P, 1], F32, name="minus_half")
         nc.vector.memset(minus_half[:], -0.5)
+        minus_quarter = const.tile([P, 1], F32, name="minus_quarter")
+        nc.vector.memset(minus_quarter[:], -0.25)
         half_pi = const.tile([P, 1], F32, name="half_pi")
         nc.vector.tensor_scalar_mul(out=half_pi[:], in0=minus_half[:], scalar1=-PI)
         minus_half_pi = const.tile([P, 1], F32, name="minus_half_pi")
         nc.vector.tensor_scalar_mul(out=minus_half_pi[:], in0=minus_half[:], scalar1=PI)
         warm = const.tile([P, 1], F32, name="warm")
-        nc.scalar.activation(out=warm[:], in_=half_pi[:], func=ACT.Sin)
+        nc.scalar.activation(out=warm[:], in_=minus_half[:], func=ACT.Sin)
 
-        step_col = sum_psum.tile([P, P], F32, name="step_col", tag="sums")
-        nc.tensor.transpose(out=step_col[:], in_=step_row[:], identity=ident[:])
-        turns = const.tile([P, N_FT], F32, name="turns")
-        nc.vector.tensor_scalar_mul(
-            out=turns[:, 0:1], in0=step_col[:, 0:1], scalar1=1.0 / (2.0 * PI)
-        )
+        step_row = const.tile([P, P], F32, name="step_row")
+        nc.vector.memset(step_row[:, 0:1], 1.0)
         w = 1
-        while w < N_FT:
+        while w < P:
             nc.vector.tensor_scalar_mul(
-                out=turns[:, w : 2 * w], in0=turns[:, 0:w], scalar1=FREQ_STEP ** (w * P // 2)
+                out=step_row[:, w : 2 * w], in0=step_row[:, 0:w], scalar1=FREQ_STEP**w
             )
             w *= 2
 
-        def nearest_whole_removed(out, value, scratch):
-            nc.vector.tensor_scalar(
+        step_col = sum_psum.tile([P, P], F32, name="step_col", tag="sums")
+        nc.tensor.transpose(out=step_col[:], in_=step_row[:], identity=ident[:])
+        turns = const.tile([P, N_FREQ], F32, name="turns")
+        for f in range(N_FREQ):
+            nc.vector.tensor_scalar_mul(
+                out=turns[:, f : f + 1], in0=step_col[:, 0:1], scalar1=FREQ_STEP ** (f * P) / (2.0 * PI)
+            )
+
+        def nearest_whole_removed(engine, out, value, scratch):
+            engine.tensor_scalar(
                 out=scratch, in0=value, scalar1=ROUND_MAGIC, scalar2=ROUND_MAGIC,
                 op0=ALU.add, op1=ALU.subtract,
             )
-            nc.vector.tensor_tensor(out=out, in0=value, in1=scratch, op=ALU.subtract)
+            engine.tensor_tensor(out=out, in0=value, in1=scratch, op=ALU.subtract)
 
-        table_shape = [P, N_FT, P]
+        table_shape = [P, N_FREQ, P]
         angle0 = const.tile(table_shape, F32, name="angle0")
         nc.vector.tensor_tensor(
             out=angle0[:],
@@ -127,70 +126,84 @@ def tile_ropemultiheadattention_pa_t_kernel(tc, x, Wq, bq, Wk, bk, out_0, out_1)
         )
         whole0 = const.tile(table_shape, F32, name="whole0")
         frac0 = const.tile(table_shape, F32, name="frac0")
-        nearest_whole_removed(frac0[:], angle0[:], whole0[:])
+        nearest_whole_removed(nc.vector, frac0[:], angle0[:], whole0[:])
 
-        block_shape = [P, N_BLOCKS, N_FT]
-        block_turns = const.tile([P, N_FT], F32, name="block_turns")
-        nc.vector.tensor_scalar_mul(out=block_turns[:], in0=turns[:], scalar1=float(P))
+        block_shape = [P, N_BLOCKS, N_FREQ]
+        block_turns = const.tile([P, N_FREQ], F32, name="block_turns")
+        nc.gpsimd.tensor_scalar(
+            out=block_turns[:], in0=turns[:], scalar1=float(P), scalar2=0.0, op0=ALU.mult, op1=ALU.add
+        )
         block_angle = const.tile(block_shape, F32, name="block_angle")
-        nc.vector.tensor_tensor(
+        nc.gpsimd.tensor_tensor(
             out=block_angle[:],
             in0=pos[:, 0:N_BLOCKS].unsqueeze(2).to_broadcast(block_shape),
             in1=block_turns[:].unsqueeze(1).to_broadcast(block_shape),
             op=ALU.mult,
         )
         block_whole = const.tile(block_shape, F32, name="block_whole")
-        shifts = const.tile([P, N_BLOCKS, N_TRIG], F32, name="shifts")
-        nearest_whole_removed(shifts[:, :, N_FT:N_TRIG], block_angle[:], block_whole[:])
-        nc.vector.tensor_scalar_add(out=shifts[:, :, 0:N_FT], in0=shifts[:, :, N_FT:N_TRIG], scalar1=-0.25)
+        shifts = const.tile([P, N_BLOCKS, 2 * N_FREQ], F32, name="shifts")
+        nearest_whole_removed(nc.gpsimd, shifts[:, :, N_FREQ : 2 * N_FREQ], block_angle[:], block_whole[:])
+        nc.gpsimd.tensor_scalar(
+            out=shifts[:, :, 0:N_FREQ], in0=shifts[:, :, N_FREQ : 2 * N_FREQ],
+            scalar1=-0.25, scalar2=0.0, op0=ALU.add, op1=ALU.add,
+        )
 
-        def group_weight(z):
-            grouped = const.tile([P, D_OUT, PACK], BF16, name="w_grouped%d" % z, align_bytes=64)
-            nc.vector.tensor_copy(
-                out=grouped[:].rearrange("p (c i) t -> p c t i", i=4),
-                in_=raw[z][:].rearrange("p t (c i) -> p c t i", i=4),
-            )
+        def group_weight(engine, z, u):
+            g, e = divmod(u, PARITIES)
+            grouped = const.tile([P, HALVES, P, PACK], BF16, name="w_grouped%d%d" % (z, u), align_bytes=64)
+            for h in range(HALVES):
+                columns = raw[z][:].rearrange(
+                    "q t (h g p e) -> q h g e p t", h=HALVES, g=GROUPS, e=PARITIES
+                )[:, h, g, e]
+                if engine is nc.vector:
+                    nc.vector.tensor_copy(
+                        out=grouped[:, h].rearrange("q (c i) t -> q c t i", i=4),
+                        in_=columns.rearrange("q (c i) t -> q c t i", i=4),
+                    )
+                else:
+                    engine.tensor_scalar(
+                        out=grouped[:, h], in0=columns, scalar1=1.0, scalar2=0.0, op0=ALU.mult, op1=ALU.add
+                    )
             return grouped
 
-        def quantise_weight(z, grouped):
-            codes = const.tile([P, D_OUT], U32, name="w_codes%d" % z, align_bytes=64)
-            scales = const.tile([P, D_OUT], U8, name="w_scales%d" % z, align_bytes=64)
+        def quantise_weight(z, u, grouped):
+            codes = const.tile([P, HALVES * P], U32, name="w_codes%d%d" % (z, u), align_bytes=64)
+            scales = const.tile([P, HALVES * P], U8, name="w_scales%d%d" % (z, u), align_bytes=64)
             nc.vector.quantize_mx(
-                out=codes[:].bitcast(FP8X4), scales=scales[:], in_=grouped[:].rearrange("p c t -> p (c t)")
+                out=codes[:].bitcast(FP8X4), scales=scales[:], in_=grouped[:].rearrange("q h p t -> q (h p t)")
             )
             return codes, scales
 
         fold_of, trig_of, x_grouped_of, x_quantised_of = {}, {}, {}, {}
 
-        def first_fold(t, tables):
+        def first_fold(t, g):
             if t not in fold_of:
-                fold_of[t] = fold_pool.tile([P, N_TRIG, P], F32, name="fold", tag="fold")
-            for i in tables:
+                fold_of[t] = fold_pool.tile([P, GROUPS, KINDS, P], F32, name="fold", tag="fold")
+            for kind in range(KINDS):
+                f = g + GROUPS * (kind % HALVES)
+                if t == 0:
+                    bias_here = 0.0 if kind >= COS else minus_quarter[:, 0:1]
+                else:
+                    row = (N_FREQ if kind >= COS else 0) + f
+                    bias_here = shifts[:, t, row : row + 1]
                 nc.scalar.activation(
-                    out=fold_of[t][:, i, :], in_=frac0[:, i % N_FT, :], func=ACT.Abs,
-                    bias=shifts[:, t, i : i + 1],
+                    out=fold_of[t][:, g, kind, :], in_=frac0[:, f, :], func=ACT.Abs, bias=bias_here
                 )
 
-        def second_fold(t, tables):
+        def second_fold(t, g):
             nc.scalar.activation(
-                out=fold_of[t][:, tables, :], in_=fold_of[t][:, tables, :], func=ACT.Abs,
-                bias=minus_half[:, 0:1],
+                out=fold_of[t][:, g], in_=fold_of[t][:, g], func=ACT.Abs, bias=minus_half[:, 0:1]
             )
 
-        def sines(t):
-            trig_of[t] = trig_pool.tile([P, N_TRIG, P], F32, name="trig", tag="trig")
+        def sines(t, g):
+            if t not in trig_of:
+                trig_of[t] = trig_pool.tile([P, GROUPS, KINDS, P], F32, name="trig", tag="trig")
             nc.scalar.activation(
-                out=trig_of[t][:, 0:HALF_FT, :], in_=fold_of[t][:, 0:HALF_FT, :], func=ACT.Sin,
+                out=trig_of[t][:, g, MINUS_SIN], in_=fold_of[t][:, g, MINUS_SIN], func=ACT.Sin,
                 scale=-2.0 * PI, bias=half_pi[:, 0:1],
             )
             nc.scalar.activation(
-                out=trig_of[t][:, HALF_FT:N_FT, :], in_=fold_of[t][:, HALF_FT:N_FT, :], func=ACT.Sin,
-                scale=2.0 * PI, bias=minus_half_pi[:, 0:1],
-            )
-
-        def cosines(t):
-            nc.scalar.activation(
-                out=trig_of[t][:, N_FT:N_TRIG, :], in_=fold_of[t][:, N_FT:N_TRIG, :], func=ACT.Sin,
+                out=trig_of[t][:, g, SIN:KINDS], in_=fold_of[t][:, g, SIN:KINDS], func=ACT.Sin,
                 scale=2.0 * PI, bias=minus_half_pi[:, 0:1],
             )
 
@@ -202,8 +215,7 @@ def tile_ropemultiheadattention_pa_t_kernel(tc, x, Wq, bq, Wk, bk, out_0, out_1)
                 words = xin[:, t, first + b, :].bitcast(F32)
                 for u in range(2):
                     nc.tensor.transpose(out=xt[:, b, u, :], in_=words[:, u : 2 * P : 2], identity=ident[:])
-            copy = nc.vector.tensor_copy if t == 0 else nc.scalar.copy
-            copy(
+            nc.scalar.copy(
                 out=x_grouped_of[t][:, first * P : (first + 2) * P, :].rearrange("w (b p) u -> w b p u", b=2),
                 in_=xt[:].rearrange("w b u p -> w b p u"),
             )
@@ -219,36 +231,39 @@ def tile_ropemultiheadattention_pa_t_kernel(tc, x, Wq, bq, Wk, bk, out_0, out_1)
             x_quantised_of[t] = (codes, scales)
 
         def prepare(t, part):
-            if part < 2:
-                turn_x(t, 2 * part)
-                first_fold(t, range(HALF_FT * part, HALF_FT * (part + 1)))
+            if part == 0:
+                turn_x(t, 0)
+            elif part == 1:
+                turn_x(t, 2)
+                first_fold(t, 0)
             elif part == 2:
                 quantise_x(t)
-                first_fold(t, range(N_FT, N_TRIG))
+                second_fold(t, 0)
             elif part == 3:
-                second_fold(t, slice(0, N_FT))
+                sines(t, 0)
             elif part == 4:
-                second_fold(t, slice(N_FT, N_TRIG))
+                first_fold(t, 1)
             elif part == 5:
-                sines(t)
+                second_fold(t, 1)
             elif part == 6:
-                cosines(t)
+                sines(t, 1)
 
         banks_of, products_of, stage_of = {}, {}, {}
         by_sequence = [P, BATCH, P]
 
         def where(k):
             t, rest = divmod(k, PAIRS_PER_BLOCK)
-            z, f = divmod(rest, HALF_FT)
-            return t, z, f
+            z, u = divmod(rest, UNITS)
+            g, e = divmod(u, PARITIES)
+            return t, z, g, e
 
         def project(k):
-            t, z, f = where(k)
+            t, z, g, e = where(k)
             x_codes, x_scales = x_quantised_of[t]
-            w_codes, w_scales = weights[z]
+            w_codes, w_scales = weights[(z, PARITIES * g + e)]
             banks = []
-            for h in range(2):
-                features = slice((f + h * HALF_FT) * P, (f + h * HALF_FT + 1) * P)
+            for h in range(HALVES):
+                features = slice(h * P, (h + 1) * P)
                 bank = mx_psum.tile([P, TOKENS], F32, name="bank", tag="bank")
                 nc.tensor.matmul_mx(
                     out=bank[:],
@@ -273,70 +288,83 @@ def tile_ropemultiheadattention_pa_t_kernel(tc, x, Wq, bq, Wk, bk, out_0, out_1)
             )
 
         def rotate(k):
-            t, z, f = where(k)
+            t, z, g, e = where(k)
             trig = trig_of[t]
-            own = prod_pool.tile([P, 2, TOKENS], F32, name="own", tag="own")
-            other = prod_pool.tile([P, 2, TOKENS], F32, name="other", tag="other")
-            for h in range(2):
-                tile_here = f + h * HALF_FT
-                tile_there = f + (1 - h) * HALF_FT
-                bias_col = bias[:, z * N_FT + tile_here : z * N_FT + tile_here + 1]
-                product(own[:, h, :], banks_of[k][h], bias_col, trig[:, N_FT + tile_here, :])
-                product(other[:, 1 - h, :], banks_of[k][h], bias_col, trig[:, tile_there, :])
+            own = prod_pool.tile([P, HALVES, TOKENS], F32, name="own", tag="own")
+            other = prod_pool.tile([P, HALVES, TOKENS], F32, name="other", tag="other")
+            for h in range(HALVES):
+                row = N_FREQ * z + GROUPS * h + g
+                bias_col = bias[:, e, row : row + 1]
+                product(own[:, h, :], banks_of[k][h], bias_col, trig[:, g, COS + h, :])
+                product(other[:, 1 - h, :], banks_of[k][h], bias_col, trig[:, g, SIN - h, :])
             products_of[k] = (own, other)
 
         def sum_and_turn(k):
-            t, z, f = where(k)
-            own, other = products_of[k]
-            if f == 0:
+            first_pair = k - k % 2 - 2
+            t, z, g, parity = where(first_pair)
+            if (t, z) not in stage_of:
                 stage_of[(t, z)] = stage_pool.tile([P, BATCH, D_OUT], F32, name="stage", tag="stage")
             stage = stage_of[(t, z)]
-            for first in range(0, BATCH, 2):
-                sums = sum_psum.tile([P, 2, 2, P], F32, name="sums", tag="sums")
-                for b in range(2):
-                    tokens = slice((first + b) * P, (first + b + 1) * P)
-                    for h in range(2):
+            last_stage = (t, z) == (N_BLOCKS - 1, 1)
+            for b in (2 * (k % 2), 2 * (k % 2) + 1):
+                tokens = slice(b * P, (b + 1) * P)
+                sums = sum_psum.tile([P, HALVES, PARITIES, P], F32, name="sums", tag="sums")
+                for e in range(PARITIES):
+                    own, other = products_of[first_pair + e]
+                    for h in range(HALVES):
                         nc.tensor.matmul(
-                            out=sums[:, b, h, :], lhsT=own[:, h, tokens], rhs=ident[:],
+                            out=sums[:, h, e, :], lhsT=own[:, h, tokens], rhs=ident[:],
                             is_transpose=True, start=True, stop=False,
                         )
                         nc.tensor.matmul(
-                            out=sums[:, b, h, :], lhsT=other[:, h, tokens], rhs=ident[:],
+                            out=sums[:, h, e, :], lhsT=other[:, h, tokens], rhs=ident[:],
                             is_transpose=True, start=False, stop=True,
                         )
+                by_group = stage[:, b, :].rearrange("p (h g c) -> p g h c", h=HALVES, g=GROUPS)[:, g]
                 nc.scalar.copy(
-                    out=stage[:, first : first + 2, :].rearrange("p b (h c) -> p b h c", h=2)[
-                        :, :, :, f * P : (f + 1) * P
-                    ],
-                    in_=sums[:],
+                    out=by_group.rearrange("p h (c e) -> p h c e", e=PARITIES),
+                    in_=sums[:].rearrange("p h e c -> p h c e"),
                 )
-            if f == HALF_FT - 1:
-                for b in range(BATCH):
-                    nc.sync.dma_start(out=outs[z][b, t * P : (t + 1) * P, :], in_=stage[:, b, :])
+                rows = outs[z][b, t * P : (t + 1) * P, :]
+                if last_stage:
+                    nc.sync.dma_start(
+                        out=rows.rearrange("p (h g c) -> p g h c", h=HALVES, g=GROUPS)[:, g], in_=by_group
+                    )
+                elif g == GROUPS - 1:
+                    nc.sync.dma_start(out=rows, in_=stage[:, b, :])
 
-        prepare(0, 0)
-        prepare(0, 1)
-        grouped_q = group_weight(0)
-        prepare(0, 2)
-        weights = [quantise_weight(0, grouped_q)]
+        bias_rows_f32 = const.tile([P, PARITIES * P], F32, name="bias_rows_f32")
+        nc.gpsimd.tensor_copy(out=bias_rows_f32[:], in_=bias_rows[:])
+        turn_x(0, 0)
+        turn_x(0, 2)
+        bias_cols = sum_psum.tile([P, PARITIES, P], F32, name="bias_cols", tag="sums")
+        for e in range(PARITIES):
+            nc.tensor.transpose(out=bias_cols[:, e, :], in_=bias_rows_f32[:, e : 2 * P : 2], identity=ident[:])
+        for g in range(GROUPS):
+            first_fold(0, g)
+            second_fold(0, g)
+            sines(0, g)
+        weights = {}
+        weights[(0, 0)] = quantise_weight(0, 0, group_weight(nc.vector, 0, 0))
+        bias = const.tile([P, PARITIES, 2 * N_FREQ], F32, name="bias")
+        nc.vector.tensor_copy(out=bias[:], in_=bias_cols[:, :, 0 : 2 * N_FREQ])
+        quantise_x(0)
         project(0)
-        for part in range(3, PAIRS_PER_BLOCK):
-            prepare(0, part)
-        bias_rows_f32 = const.tile([P, P], F32, name="bias_rows_f32")
-        nc.vector.tensor_copy(out=bias_rows_f32[:], in_=bias_rows[:])
-        bias_cols = sum_psum.tile([P, P], F32, name="bias_cols", tag="sums")
-        nc.tensor.transpose(out=bias_cols[:], in_=bias_rows_f32[:], identity=ident[:])
-        bias = const.tile([P, 2 * N_FT], F32, name="bias")
-        nc.vector.tensor_copy(out=bias[:], in_=bias_cols[:, 0 : 2 * N_FT])
-        weights.append(quantise_weight(1, group_weight(1)))
+        weights[(0, 1)] = quantise_weight(0, 1, group_weight(nc.vector, 0, 1))
+        grouped_of = {}
+        for n in range(2, 2 * UNITS):
+            z, u = divmod(n, UNITS)
+            grouped_of[n] = group_weight(nc.gpsimd, z, u)
 
-        for k in range(N_PAIRS + 1):
+        for k in range(N_PAIRS + 2):
             if k + 1 < N_PAIRS:
                 project(k + 1)
+            if k + 2 in grouped_of:
+                weights[divmod(k + 2, UNITS)] = quantise_weight(*divmod(k + 2, UNITS), grouped_of[k + 2])
             if k < N_PAIRS:
                 rotate(k)
-            if k >= 1:
-                sum_and_turn(k - 1)
+            if k >= 2:
+                sum_and_turn(k)
             t, part = divmod(k, PAIRS_PER_BLOCK)
             if t + 1 < N_BLOCKS:
                 prepare(t + 1, part)

@@ -45,6 +45,7 @@ def tile_ropemultiheadattention_pa_t_kernel(tc, x, Wq, bq, Wk, bk, out_0, out_1)
         fold_pool = ctx.enter_context(tc.tile_pool(name="fold", bufs=1))
         trig_pool = ctx.enter_context(tc.tile_pool(name="trig", bufs=2))
         prod_pool = ctx.enter_context(tc.tile_pool(name="prod", bufs=5))
+        value_pool = ctx.enter_context(tc.tile_pool(name="value", bufs=2))
         stage_pool = ctx.enter_context(tc.tile_pool(name="stage", bufs=3))
         mx_psum = ctx.enter_context(tc.psum_pool(name="mx_psum", bufs=4))
         sum_psum = ctx.enter_context(tc.psum_pool(name="sum_psum", bufs=3))
@@ -287,6 +288,9 @@ def tile_ropemultiheadattention_pa_t_kernel(tc, x, Wq, bq, Wk, bk, out_0, out_1)
                 op1=ALU.mult,
             )
 
+        def on_gpsimd(t, e, h):
+            return t > 0 and e == 0 and h == 0
+
         def rotate(k):
             t, z, g, e = where(k)
             trig = trig_of[t]
@@ -295,8 +299,20 @@ def tile_ropemultiheadattention_pa_t_kernel(tc, x, Wq, bq, Wk, bk, out_0, out_1)
             for h in range(HALVES):
                 row = N_FREQ * z + GROUPS * h + g
                 bias_col = bias[:, e, row : row + 1]
-                product(own[:, h, :], banks_of[k][h], bias_col, trig[:, g, COS + h, :])
-                product(other[:, 1 - h, :], banks_of[k][h], bias_col, trig[:, g, SIN - h, :])
+                targets = ((own[:, h, :], trig[:, g, COS + h, :]), (other[:, 1 - h, :], trig[:, g, SIN - h, :]))
+                if on_gpsimd(t, e, h):
+                    value = value_pool.tile([P, TOKENS], F32, name="value", tag="value")
+                    nc.scalar.activation(out=value[:], in_=banks_of[k][h][:], func=ACT.Identity, bias=bias_col)
+                    for out, table in targets:
+                        nc.gpsimd.tensor_tensor(
+                            out=out.rearrange("f (b p) -> f b p", b=BATCH),
+                            in0=value[:].rearrange("f (b p) -> f b p", b=BATCH),
+                            in1=table.unsqueeze(1).to_broadcast(by_sequence),
+                            op=ALU.mult,
+                        )
+                else:
+                    for out, table in targets:
+                        product(out, banks_of[k][h], bias_col, table)
             products_of[k] = (own, other)
 
         def sum_and_turn(k):

@@ -32,6 +32,9 @@ MINUS_SIN, SIN, COS, KINDS = 0, 1, 2, 4
 FREQ_STEP = ROPE_BASE ** (-2.0 / D_OUT)
 ROUND_MAGIC = 12582912.0
 
+FIRST_SHARED_QUAD = 2
+TURN_LAG = 3
+
 FLOPS = 2 * BATCH * SEQ * D_IN * 2 * D_OUT
 
 
@@ -44,7 +47,7 @@ def tile_ropemultiheadattention_pa_t_kernel(tc, x, Wq, bq, Wk, bk, out_0, out_1)
         xq_pool = ctx.enter_context(tc.tile_pool(name="xq", bufs=2))
         fold_pool = ctx.enter_context(tc.tile_pool(name="fold", bufs=1))
         trig_pool = ctx.enter_context(tc.tile_pool(name="trig", bufs=2))
-        prod_pool = ctx.enter_context(tc.tile_pool(name="prod", bufs=5))
+        prod_pool = ctx.enter_context(tc.tile_pool(name="prod", bufs=7))
         value_pool = ctx.enter_context(tc.tile_pool(name="value", bufs=2))
         stage_pool = ctx.enter_context(tc.tile_pool(name="stage", bufs=3))
         mx_psum = ctx.enter_context(tc.psum_pool(name="mx_psum", bufs=4))
@@ -288,8 +291,15 @@ def tile_ropemultiheadattention_pa_t_kernel(tc, x, Wq, bq, Wk, bk, out_0, out_1)
                 op1=ALU.mult,
             )
 
-        def on_gpsimd(t, e, h):
-            return t > 0 and e == 0 and h == 0
+        def multiplied_on_gpsimd(k, h):
+            quad, e = divmod(k, PARITIES)
+            return quad >= FIRST_SHARED_QUAD and quad % 2 == 0 and (e, h) == (0, 0)
+
+        def added_on_gpsimd(k, h):
+            quad, e = divmod(k, PARITIES)
+            if quad < FIRST_SHARED_QUAD:
+                return False
+            return (e, h) == (0, 0) if quad % 2 == 0 else (e, h) != (1, 1)
 
         def rotate(k):
             t, z, g, e = where(k)
@@ -300,7 +310,7 @@ def tile_ropemultiheadattention_pa_t_kernel(tc, x, Wq, bq, Wk, bk, out_0, out_1)
                 row = N_FREQ * z + GROUPS * h + g
                 bias_col = bias[:, e, row : row + 1]
                 targets = ((own[:, h, :], trig[:, g, COS + h, :]), (other[:, 1 - h, :], trig[:, g, SIN - h, :]))
-                if on_gpsimd(t, e, h):
+                if multiplied_on_gpsimd(k, h):
                     value = value_pool.tile([P, TOKENS], F32, name="value", tag="value")
                     nc.scalar.activation(out=value[:], in_=banks_of[k][h][:], func=ACT.Identity, bias=bias_col)
                     for out, table in targets:
@@ -313,10 +323,13 @@ def tile_ropemultiheadattention_pa_t_kernel(tc, x, Wq, bq, Wk, bk, out_0, out_1)
                 else:
                     for out, table in targets:
                         product(out, banks_of[k][h], bias_col, table)
+            for h in range(HALVES):
+                if added_on_gpsimd(k, h):
+                    nc.gpsimd.tensor_tensor(out=own[:, h, :], in0=own[:, h, :], in1=other[:, h, :], op=ALU.add)
             products_of[k] = (own, other)
 
         def sum_and_turn(k):
-            first_pair = k - k % 2 - 2
+            first_pair = k - k % 2
             t, z, g, parity = where(first_pair)
             if (t, z) not in stage_of:
                 stage_of[(t, z)] = stage_pool.tile([P, BATCH, D_OUT], F32, name="stage", tag="stage")
@@ -328,14 +341,16 @@ def tile_ropemultiheadattention_pa_t_kernel(tc, x, Wq, bq, Wk, bk, out_0, out_1)
                 for e in range(PARITIES):
                     own, other = products_of[first_pair + e]
                     for h in range(HALVES):
+                        whole = added_on_gpsimd(first_pair + e, h)
                         nc.tensor.matmul(
                             out=sums[:, h, e, :], lhsT=own[:, h, tokens], rhs=ident[:],
-                            is_transpose=True, start=True, stop=False,
+                            is_transpose=True, start=True, stop=whole,
                         )
-                        nc.tensor.matmul(
-                            out=sums[:, h, e, :], lhsT=other[:, h, tokens], rhs=ident[:],
-                            is_transpose=True, start=False, stop=True,
-                        )
+                        if not whole:
+                            nc.tensor.matmul(
+                                out=sums[:, h, e, :], lhsT=other[:, h, tokens], rhs=ident[:],
+                                is_transpose=True, start=False, stop=True,
+                            )
                 by_group = stage[:, b, :].rearrange("p (h g c) -> p g h c", h=HALVES, g=GROUPS)[:, g]
                 nc.scalar.copy(
                     out=by_group.rearrange("p h (c e) -> p h c e", e=PARITIES),
@@ -372,15 +387,15 @@ def tile_ropemultiheadattention_pa_t_kernel(tc, x, Wq, bq, Wk, bk, out_0, out_1)
             z, u = divmod(n, UNITS)
             grouped_of[n] = group_weight(nc.gpsimd, z, u)
 
-        for k in range(N_PAIRS + 2):
+        for k in range(N_PAIRS + TURN_LAG):
             if k + 1 < N_PAIRS:
                 project(k + 1)
             if k + 2 in grouped_of:
                 weights[divmod(k + 2, UNITS)] = quantise_weight(*divmod(k + 2, UNITS), grouped_of[k + 2])
             if k < N_PAIRS:
                 rotate(k)
-            if k >= 2:
-                sum_and_turn(k)
+            if k >= TURN_LAG:
+                sum_and_turn(k - TURN_LAG)
             t, part = divmod(k, PAIRS_PER_BLOCK)
             if t + 1 < N_BLOCKS:
                 prepare(t + 1, part)

@@ -33,6 +33,9 @@ FREQ_STEP = ROPE_BASE ** (-2.0 / D_OUT)
 ROUND_MAGIC = 12582912.0
 
 FIRST_SHARED_QUAD = 2
+SHARED_QUADS = N_PAIRS // PARITIES - 1
+ADDED, MULTIPLIED = 0, 1
+MULTIPLY_EVERY = 2
 TURN_LAG = 3
 
 FLOPS = 2 * BATCH * SEQ * D_IN * 2 * D_OUT
@@ -45,9 +48,10 @@ def tile_ropemultiheadattention_pa_t_kernel(tc, x, Wq, bq, Wk, bk, out_0, out_1)
         ctx.enter_context(tc.manual_schedule())
         const = ctx.enter_context(tc.tile_pool(name="const", bufs=1))
         xq_pool = ctx.enter_context(tc.tile_pool(name="xq", bufs=2))
+        xw_pool = ctx.enter_context(tc.tile_pool(name="xw", bufs=2))
         fold_pool = ctx.enter_context(tc.tile_pool(name="fold", bufs=1))
         trig_pool = ctx.enter_context(tc.tile_pool(name="trig", bufs=2))
-        prod_pool = ctx.enter_context(tc.tile_pool(name="prod", bufs=7))
+        prod_pool = ctx.enter_context(tc.tile_pool(name="prod", bufs=8))
         value_pool = ctx.enter_context(tc.tile_pool(name="value", bufs=2))
         stage_pool = ctx.enter_context(tc.tile_pool(name="stage", bufs=3))
         mx_psum = ctx.enter_context(tc.psum_pool(name="mx_psum", bufs=4))
@@ -178,7 +182,7 @@ def tile_ropemultiheadattention_pa_t_kernel(tc, x, Wq, bq, Wk, bk, out_0, out_1)
             )
             return codes, scales
 
-        fold_of, trig_of, x_grouped_of, x_quantised_of = {}, {}, {}, {}
+        fold_of, trig_of, x_words_of, x_grouped_of, x_quantised_of = {}, {}, {}, {}, {}
 
         def first_fold(t, g):
             if t not in fold_of:
@@ -211,14 +215,26 @@ def tile_ropemultiheadattention_pa_t_kernel(tc, x, Wq, bq, Wk, bk, out_0, out_1)
                 scale=2.0 * PI, bias=minus_half_pi[:, 0:1],
             )
 
+        def separate_words(t, first):
+            if first == 0:
+                x_words_of[t] = xw_pool.tile([P, BATCH, 2, P], F32, name="x_words", tag="x_words")
+            two = slice(first, first + 2)
+            nc.scalar.copy(
+                out=x_words_of[t][:, two],
+                in_=xin[:, t, two, :].rearrange("p b k -> p (b k)").bitcast(F32).rearrange("p (b w u) -> p b u w", b=2, u=2),
+            )
+
         def turn_x(t, first):
             if first == 0:
                 x_grouped_of[t] = xq_pool.tile([P, TOKENS, 2], F32, name="x_grouped", tag="x_grouped", align_bytes=64)
             xt = xt_psum.tile([P, 2, 2, P], F32, name="xt", tag="xt")
             for b in range(2):
-                words = xin[:, t, first + b, :].bitcast(F32)
                 for u in range(2):
-                    nc.tensor.transpose(out=xt[:, b, u, :], in_=words[:, u : 2 * P : 2], identity=ident[:])
+                    if t == 0:
+                        words = xin[:, t, first + b, :].bitcast(F32)[:, u : 2 * P : 2]
+                    else:
+                        words = x_words_of[t][:, first + b, u, :]
+                    nc.tensor.transpose(out=xt[:, b, u, :], in_=words, identity=ident[:])
             nc.scalar.copy(
                 out=x_grouped_of[t][:, first * P : (first + 2) * P, :].rearrange("w (b p) u -> w b p u", b=2),
                 in_=xt[:].rearrange("w b u p -> w b p u"),
@@ -236,16 +252,18 @@ def tile_ropemultiheadattention_pa_t_kernel(tc, x, Wq, bq, Wk, bk, out_0, out_1)
 
         def prepare(t, part):
             if part == 0:
-                turn_x(t, 0)
-            elif part == 1:
-                turn_x(t, 2)
+                separate_words(t, 0)
                 first_fold(t, 0)
+            elif part == 1:
+                separate_words(t, 2)
+                turn_x(t, 0)
             elif part == 2:
-                quantise_x(t)
                 second_fold(t, 0)
+                turn_x(t, 2)
             elif part == 3:
                 sines(t, 0)
             elif part == 4:
+                quantise_x(t)
                 first_fold(t, 1)
             elif part == 5:
                 second_fold(t, 1)
@@ -253,7 +271,6 @@ def tile_ropemultiheadattention_pa_t_kernel(tc, x, Wq, bq, Wk, bk, out_0, out_1)
                 sines(t, 1)
 
         banks_of, products_of, stage_of = {}, {}, {}
-        by_sequence = [P, BATCH, P]
 
         def where(k):
             t, rest = divmod(k, PAIRS_PER_BLOCK)
@@ -281,52 +298,55 @@ def tile_ropemultiheadattention_pa_t_kernel(tc, x, Wq, bq, Wk, bk, out_0, out_1)
                 banks.append(bank)
             banks_of[k] = banks
 
-        def product(out, bank, bias_col, table):
-            nc.vector.scalar_tensor_tensor(
-                out=out.rearrange("f (b p) -> f b p", b=BATCH),
-                in0=bank[:].rearrange("f (b p) -> f b p", b=BATCH),
-                scalar=bias_col,
-                in1=table.unsqueeze(1).to_broadcast(by_sequence),
-                op0=ALU.add,
-                op1=ALU.mult,
-            )
+        def shared(k):
+            return FIRST_SHARED_QUAD <= k // PARITIES < SHARED_QUADS
 
         def multiplied_on_gpsimd(k, h):
-            quad, e = divmod(k, PARITIES)
-            return quad >= FIRST_SHARED_QUAD and quad % 2 == 0 and (e, h) == (0, 0)
+            return shared(k) and (k // PARITIES) % MULTIPLY_EVERY == 0 and (k % PARITIES, h) == (MULTIPLIED, 0)
 
-        def added_on_gpsimd(k, h):
-            quad, e = divmod(k, PARITIES)
-            if quad < FIRST_SHARED_QUAD:
-                return False
-            return (e, h) == (0, 0) if quad % 2 == 0 else (e, h) != (1, 1)
+        def added_on_gpsimd(k):
+            return shared(k) and k % PARITIES == ADDED
 
-        def rotate(k):
+        two_tables = [P, 2, BATCH, P]
+
+        def factors(k, h):
             t, z, g, e = where(k)
-            trig = trig_of[t]
-            own = prod_pool.tile([P, HALVES, TOKENS], F32, name="own", tag="own")
-            other = prod_pool.tile([P, HALVES, TOKENS], F32, name="other", tag="other")
+            if k not in products_of:
+                products_of[k] = prod_pool.tile([P, KINDS, TOKENS], F32, name="products", tag="products")
+            kinds = slice(SIN, COS + 1) if h == 0 else slice(MINUS_SIN, KINDS, KINDS - 1)
+            out = products_of[k][:, kinds, :].rearrange("f n (b p) -> f n b p", b=BATCH)
+            return out, trig_of[t][:, g, kinds, :].unsqueeze(2).to_broadcast(two_tables)
+
+        def twice(tile):
+            return tile[:].rearrange("f (b p) -> f b p", b=BATCH).unsqueeze(1).to_broadcast(two_tables)
+
+        def bias_col(k, h):
+            t, z, g, e = where(k)
+            row = N_FREQ * z + GROUPS * h + g
+            return bias[:, e, row : row + 1]
+
+        def multiply_share(k):
             for h in range(HALVES):
-                row = N_FREQ * z + GROUPS * h + g
-                bias_col = bias[:, e, row : row + 1]
-                targets = ((own[:, h, :], trig[:, g, COS + h, :]), (other[:, 1 - h, :], trig[:, g, SIN - h, :]))
                 if multiplied_on_gpsimd(k, h):
                     value = value_pool.tile([P, TOKENS], F32, name="value", tag="value")
-                    nc.scalar.activation(out=value[:], in_=banks_of[k][h][:], func=ACT.Identity, bias=bias_col)
-                    for out, table in targets:
-                        nc.gpsimd.tensor_tensor(
-                            out=out.rearrange("f (b p) -> f b p", b=BATCH),
-                            in0=value[:].rearrange("f (b p) -> f b p", b=BATCH),
-                            in1=table.unsqueeze(1).to_broadcast(by_sequence),
-                            op=ALU.mult,
-                        )
-                else:
-                    for out, table in targets:
-                        product(out, banks_of[k][h], bias_col, table)
+                    nc.scalar.activation(out=value[:], in_=banks_of[k][h][:], func=ACT.Identity, bias=bias_col(k, h))
+                    out, tables = factors(k, h)
+                    nc.gpsimd.tensor_tensor(out=out, in0=twice(value), in1=tables, op=ALU.mult)
+
+        def rotate(k):
             for h in range(HALVES):
-                if added_on_gpsimd(k, h):
-                    nc.gpsimd.tensor_tensor(out=own[:, h, :], in0=own[:, h, :], in1=other[:, h, :], op=ALU.add)
-            products_of[k] = (own, other)
+                if not multiplied_on_gpsimd(k, h):
+                    out, tables = factors(k, h)
+                    for n in range(2):
+                        nc.vector.scalar_tensor_tensor(
+                            out=out[:, n], in0=banks_of[k][h][:].rearrange("f (b p) -> f b p", b=BATCH),
+                            scalar=bias_col(k, h), in1=tables[:, n], op0=ALU.add, op1=ALU.mult,
+                        )
+
+        def add_share(k):
+            if added_on_gpsimd(k):
+                own, other = products_of[k][:, COS:KINDS, :], products_of[k][:, MINUS_SIN:COS, :]
+                nc.gpsimd.tensor_tensor(out=own, in0=own, in1=other, op=ALU.add)
 
         def sum_and_turn(k):
             first_pair = k - k % 2
@@ -339,16 +359,16 @@ def tile_ropemultiheadattention_pa_t_kernel(tc, x, Wq, bq, Wk, bk, out_0, out_1)
                 tokens = slice(b * P, (b + 1) * P)
                 sums = sum_psum.tile([P, HALVES, PARITIES, P], F32, name="sums", tag="sums")
                 for e in range(PARITIES):
-                    own, other = products_of[first_pair + e]
+                    products = products_of[first_pair + e]
+                    whole = added_on_gpsimd(first_pair + e)
                     for h in range(HALVES):
-                        whole = added_on_gpsimd(first_pair + e, h)
                         nc.tensor.matmul(
-                            out=sums[:, h, e, :], lhsT=own[:, h, tokens], rhs=ident[:],
+                            out=sums[:, h, e, :], lhsT=products[:, COS + h, tokens], rhs=ident[:],
                             is_transpose=True, start=True, stop=whole,
                         )
                         if not whole:
                             nc.tensor.matmul(
-                                out=sums[:, h, e, :], lhsT=other[:, h, tokens], rhs=ident[:],
+                                out=sums[:, h, e, :], lhsT=products[:, MINUS_SIN + h, tokens], rhs=ident[:],
                                 is_transpose=True, start=False, stop=True,
                             )
                 by_group = stage[:, b, :].rearrange("p (h g c) -> p g h c", h=HALVES, g=GROUPS)[:, g]
@@ -392,8 +412,11 @@ def tile_ropemultiheadattention_pa_t_kernel(tc, x, Wq, bq, Wk, bk, out_0, out_1)
                 project(k + 1)
             if k + 2 in grouped_of:
                 weights[divmod(k + 2, UNITS)] = quantise_weight(*divmod(k + 2, UNITS), grouped_of[k + 2])
+            if k + 1 < N_PAIRS:
+                multiply_share(k + 1)
             if k < N_PAIRS:
                 rotate(k)
+                add_share(k)
             if k >= TURN_LAG:
                 sum_and_turn(k - TURN_LAG)
             t, part = divmod(k, PAIRS_PER_BLOCK)

@@ -35,7 +35,7 @@ ROUND_MAGIC = 12582912.0
 FIRST_SHARED_QUAD = 2
 SHARED_QUADS = N_PAIRS // PARITIES - 1
 ADDED, MULTIPLIED = 0, 1
-MULTIPLY_EVERY = 2
+MULTIPLY_EVERY = 3
 TURN_LAG = 3
 
 FLOPS = 2 * BATCH * SEQ * D_IN * 2 * D_OUT
@@ -305,7 +305,7 @@ def tile_ropemultiheadattention_pa_t_kernel(tc, x, Wq, bq, Wk, bk, out_0, out_1)
             return shared(k) and (k // PARITIES) % MULTIPLY_EVERY == 0 and (k % PARITIES, h) == (MULTIPLIED, 0)
 
         def added_on_gpsimd(k):
-            return shared(k) and k % PARITIES == ADDED
+            return shared(k) and (k // PARITIES) % MULTIPLY_EVERY != 0 and k % PARITIES == ADDED
 
         two_tables = [P, 2, BATCH, P]
 

@@ -35,8 +35,12 @@ ROUND_MAGIC = 12582912.0
 FIRST_SHARED_QUAD = 2
 SHARED_QUADS = N_PAIRS // PARITIES - 1
 ADDED, MULTIPLIED = 0, 1
-MULTIPLY_EVERY = 3
+MULTIPLIED_QUADS = (0, 3)
+ADDED_QUADS = (0, 1, 2)
+QUANTISE_STEP = 4
 TURN_LAG = 3
+
+GROUPED_ON_SCALAR = (2, 3)
 
 FLOPS = 2 * BATCH * SEQ * D_IN * 2 * D_OUT
 
@@ -49,14 +53,13 @@ def tile_ropemultiheadattention_pa_t_kernel(tc, x, Wq, bq, Wk, bk, out_0, out_1)
         const = ctx.enter_context(tc.tile_pool(name="const", bufs=1))
         xq_pool = ctx.enter_context(tc.tile_pool(name="xq", bufs=2))
         xw_pool = ctx.enter_context(tc.tile_pool(name="xw", bufs=2))
-        fold_pool = ctx.enter_context(tc.tile_pool(name="fold", bufs=1))
+        fold_pool = ctx.enter_context(tc.tile_pool(name="fold", bufs=2))
         trig_pool = ctx.enter_context(tc.tile_pool(name="trig", bufs=2))
         prod_pool = ctx.enter_context(tc.tile_pool(name="prod", bufs=8))
         value_pool = ctx.enter_context(tc.tile_pool(name="value", bufs=2))
         stage_pool = ctx.enter_context(tc.tile_pool(name="stage", bufs=3))
-        mx_psum = ctx.enter_context(tc.psum_pool(name="mx_psum", bufs=4))
+        mx_psum = ctx.enter_context(tc.psum_pool(name="mx_psum", bufs=5))
         sum_psum = ctx.enter_context(tc.psum_pool(name="sum_psum", bufs=3))
-        xt_psum = ctx.enter_context(tc.psum_pool(name="xt_psum", bufs=1))
 
         xin = const.tile([P, N_BLOCKS, BATCH, D_IN], BF16, name="xin")
 
@@ -149,12 +152,47 @@ def tile_ropemultiheadattention_pa_t_kernel(tc, x, Wq, bq, Wk, bk, out_0, out_1)
             op=ALU.mult,
         )
         block_whole = const.tile(block_shape, F32, name="block_whole")
-        shifts = const.tile([P, N_BLOCKS, 2 * N_FREQ], F32, name="shifts")
-        nearest_whole_removed(nc.gpsimd, shifts[:, :, N_FREQ : 2 * N_FREQ], block_angle[:], block_whole[:])
-        nc.gpsimd.tensor_scalar(
-            out=shifts[:, :, 0:N_FREQ], in0=shifts[:, :, N_FREQ : 2 * N_FREQ],
-            scalar1=-0.25, scalar2=0.0, op0=ALU.add, op1=ALU.add,
-        )
+        block_frac = const.tile(block_shape, F32, name="block_frac")
+        nearest_whole_removed(nc.gpsimd, block_frac[:], block_angle[:], block_whole[:])
+        bias_rows_f32 = const.tile([P, PARITIES * P], F32, name="bias_rows_f32")
+        nc.gpsimd.tensor_copy(out=bias_rows_f32[:], in_=bias_rows[:])
+        column_shape = [P, N_BLOCKS, KINDS * GROUPS]
+
+        def column_tile(name):
+            return const.tile(column_shape, F32, name=name)
+
+        def of_kind(tile, kind, count=1):
+            return tile[:, :, kind * GROUPS : (kind + count) * GROUPS]
+
+        def affine(out, value, factor, addend):
+            nc.gpsimd.tensor_scalar(
+                out=out, in0=value, scalar1=factor, scalar2=addend, op0=ALU.mult, op1=ALU.add
+            )
+
+        half_turns = column_tile("half_turns")
+        lower, upper = block_frac[:, :, 0:GROUPS], block_frac[:, :, GROUPS:N_FREQ]
+        affine(of_kind(half_turns, MINUS_SIN), lower, 2.0, -0.5)
+        affine(of_kind(half_turns, SIN), upper, 2.0, 0.0)
+        affine(of_kind(half_turns, COS), lower, 2.0, 0.0)
+        affine(of_kind(half_turns, COS + 1), upper, 2.0, 0.5)
+        half_whole = column_tile("half_whole")
+        half_frac = column_tile("half_frac")
+        nearest_whole_removed(nc.gpsimd, half_frac[:], half_turns[:], half_whole[:])
+        pairs = column_tile("pairs")
+        affine(pairs[:], half_whole[:], 0.5, 0.0)
+        pairs_whole = column_tile("pairs_whole")
+        pairs_frac = column_tile("pairs_frac")
+        nearest_whole_removed(nc.gpsimd, pairs_frac[:], pairs[:], pairs_whole[:])
+        sign = column_tile("sign")
+        nc.gpsimd.tensor_tensor(out=sign[:], in0=pairs_frac[:], in1=pairs_frac[:], op=ALU.mult)
+        affine(sign[:], sign[:], -8.0, 1.0)
+        turn_shift, sine_scale, sine_bias = column_tile("turn_shift"), column_tile("sine_scale"), column_tile("sine_bias")
+        affine(turn_shift[:], half_frac[:], 0.5, 0.0)
+        affine(sine_scale[:], sign[:], 2.0 * PI, 0.0)
+        affine(of_kind(sine_scale, COS), of_kind(sign, COS), -2.0 * PI, 0.0)
+        nc.gpsimd.tensor_tensor(out=sine_bias[:], in0=sine_scale[:], in1=turn_shift[:], op=ALU.mult)
+        for kind in (MINUS_SIN, COS):
+            affine(of_kind(sine_bias, kind), of_kind(sine_scale, kind), -0.25, 0.0)
 
         def group_weight(engine, z, u):
             g, e = divmod(u, PARITIES)
@@ -168,6 +206,8 @@ def tile_ropemultiheadattention_pa_t_kernel(tc, x, Wq, bq, Wk, bk, out_0, out_1)
                         out=grouped[:, h].rearrange("q (c i) t -> q c t i", i=4),
                         in_=columns.rearrange("q (c i) t -> q c t i", i=4),
                     )
+                elif engine is nc.scalar:
+                    engine.copy(out=grouped[:, h], in_=columns)
                 else:
                     engine.tensor_scalar(
                         out=grouped[:, h], in0=columns, scalar1=1.0, scalar2=0.0, op0=ALU.mult, op1=ALU.add
@@ -184,36 +224,27 @@ def tile_ropemultiheadattention_pa_t_kernel(tc, x, Wq, bq, Wk, bk, out_0, out_1)
 
         fold_of, trig_of, x_words_of, x_grouped_of, x_quantised_of = {}, {}, {}, {}, {}
 
-        def first_fold(t, g):
-            if t not in fold_of:
-                fold_of[t] = fold_pool.tile([P, GROUPS, KINDS, P], F32, name="fold", tag="fold")
-            for kind in range(KINDS):
-                f = g + GROUPS * (kind % HALVES)
-                if t == 0:
-                    bias_here = 0.0 if kind >= COS else minus_quarter[:, 0:1]
-                else:
-                    row = (N_FREQ if kind >= COS else 0) + f
-                    bias_here = shifts[:, t, row : row + 1]
-                nc.scalar.activation(
-                    out=fold_of[t][:, g, kind, :], in_=frac0[:, f, :], func=ACT.Abs, bias=bias_here
-                )
+        def folds(t, g):
+            fold_of[(t, g)] = fold_pool.tile([P, 2, P], F32, name="fold", tag="fold")
+            for n, kind in enumerate((MINUS_SIN, COS)):
+                column = kind * GROUPS + g
+                shift = turn_shift[:, t, column : column + 1] if t else (minus_quarter[:, 0:1], 0.0)[n]
+                nc.scalar.activation(out=fold_of[(t, g)][:, n, :], in_=frac0[:, g, :], func=ACT.Abs, bias=shift)
 
-        def second_fold(t, g):
-            nc.scalar.activation(
-                out=fold_of[t][:, g], in_=fold_of[t][:, g], func=ACT.Abs, bias=minus_half[:, 0:1]
-            )
-
-        def sines(t, g):
+        def sines(t, g, kinds):
             if t not in trig_of:
                 trig_of[t] = trig_pool.tile([P, GROUPS, KINDS, P], F32, name="trig", tag="trig")
-            nc.scalar.activation(
-                out=trig_of[t][:, g, MINUS_SIN], in_=fold_of[t][:, g, MINUS_SIN], func=ACT.Sin,
-                scale=-2.0 * PI, bias=half_pi[:, 0:1],
-            )
-            nc.scalar.activation(
-                out=trig_of[t][:, g, SIN:KINDS], in_=fold_of[t][:, g, SIN:KINDS], func=ACT.Sin,
-                scale=2.0 * PI, bias=minus_half_pi[:, 0:1],
-            )
+            for kind in kinds:
+                column = kind * GROUPS + g
+                if t:
+                    scale, bias_here = sine_scale[:, t, column : column + 1], sine_bias[:, t, column : column + 1]
+                else:
+                    scale = -2.0 * PI if kind == COS else 2.0 * PI
+                    bias_here = {MINUS_SIN: minus_half_pi[:, 0:1], SIN: 0.0}.get(kind, half_pi[:, 0:1])
+                source = frac0[:, g + GROUPS, :] if kind % 2 else fold_of[(t, g)][:, kind // 2, :]
+                nc.scalar.activation(
+                    out=trig_of[t][:, g, kind], in_=source, func=ACT.Sin, scale=scale, bias=bias_here
+                )
 
         def separate_words(t, first):
             if first == 0:
@@ -227,7 +258,7 @@ def tile_ropemultiheadattention_pa_t_kernel(tc, x, Wq, bq, Wk, bk, out_0, out_1)
         def turn_x(t, first):
             if first == 0:
                 x_grouped_of[t] = xq_pool.tile([P, TOKENS, 2], F32, name="x_grouped", tag="x_grouped", align_bytes=64)
-            xt = xt_psum.tile([P, 2, 2, P], F32, name="xt", tag="xt")
+            xt = sum_psum.tile([P, 2, 2, P], F32, name="xt", tag="sums")
             for b in range(2):
                 for u in range(2):
                     if t == 0:
@@ -253,22 +284,22 @@ def tile_ropemultiheadattention_pa_t_kernel(tc, x, Wq, bq, Wk, bk, out_0, out_1)
         def prepare(t, part):
             if part == 0:
                 separate_words(t, 0)
-                first_fold(t, 0)
             elif part == 1:
                 separate_words(t, 2)
                 turn_x(t, 0)
             elif part == 2:
-                second_fold(t, 0)
+                folds(t, 0)
                 turn_x(t, 2)
             elif part == 3:
-                sines(t, 0)
+                sines(t, 0, (MINUS_SIN, COS))
             elif part == 4:
-                quantise_x(t)
-                first_fold(t, 1)
+                sines(t, 0, (SIN, COS + 1))
             elif part == 5:
-                second_fold(t, 1)
+                folds(t, 1)
             elif part == 6:
-                sines(t, 1)
+                sines(t, 1, (MINUS_SIN, COS))
+            elif part == 7:
+                sines(t, 1, (SIN, COS + 1))
 
         banks_of, products_of, stage_of = {}, {}, {}
 
@@ -301,11 +332,14 @@ def tile_ropemultiheadattention_pa_t_kernel(tc, x, Wq, bq, Wk, bk, out_0, out_1)
         def shared(k):
             return FIRST_SHARED_QUAD <= k // PARITIES < SHARED_QUADS
 
+        def quad_of_block(k):
+            return k % PAIRS_PER_BLOCK // PARITIES
+
         def multiplied_on_gpsimd(k, h):
-            return shared(k) and (k // PARITIES) % MULTIPLY_EVERY == 0 and (k % PARITIES, h) == (MULTIPLIED, 0)
+            return shared(k) and quad_of_block(k) in MULTIPLIED_QUADS and (k % PARITIES, h) == (MULTIPLIED, 0)
 
         def added_on_gpsimd(k):
-            return shared(k) and (k // PARITIES) % MULTIPLY_EVERY != 0 and k % PARITIES == ADDED
+            return shared(k) and quad_of_block(k) in ADDED_QUADS and k % PARITIES == ADDED
 
         two_tables = [P, 2, BATCH, P]
 
@@ -342,6 +376,9 @@ def tile_ropemultiheadattention_pa_t_kernel(tc, x, Wq, bq, Wk, bk, out_0, out_1)
                             out=out[:, n], in0=banks_of[k][h][:].rearrange("f (b p) -> f b p", b=BATCH),
                             scalar=bias_col(k, h), in1=tables[:, n], op0=ALU.add, op1=ALU.mult,
                         )
+                t, part = divmod(k, PAIRS_PER_BLOCK)
+                if h == 0 and part == QUANTISE_STEP and t + 1 < N_BLOCKS:
+                    quantise_x(t + 1)
 
         def add_share(k):
             if added_on_gpsimd(k):
@@ -384,17 +421,14 @@ def tile_ropemultiheadattention_pa_t_kernel(tc, x, Wq, bq, Wk, bk, out_0, out_1)
                 elif g == GROUPS - 1:
                     nc.sync.dma_start(out=rows, in_=stage[:, b, :])
 
-        bias_rows_f32 = const.tile([P, PARITIES * P], F32, name="bias_rows_f32")
-        nc.gpsimd.tensor_copy(out=bias_rows_f32[:], in_=bias_rows[:])
         turn_x(0, 0)
         turn_x(0, 2)
         bias_cols = sum_psum.tile([P, PARITIES, P], F32, name="bias_cols", tag="sums")
         for e in range(PARITIES):
             nc.tensor.transpose(out=bias_cols[:, e, :], in_=bias_rows_f32[:, e : 2 * P : 2], identity=ident[:])
         for g in range(GROUPS):
-            first_fold(0, g)
-            second_fold(0, g)
-            sines(0, g)
+            folds(0, g)
+            sines(0, g, range(KINDS))
         weights = {}
         weights[(0, 0)] = quantise_weight(0, 0, group_weight(nc.vector, 0, 0))
         bias = const.tile([P, PARITIES, 2 * N_FREQ], F32, name="bias")
@@ -405,7 +439,7 @@ def tile_ropemultiheadattention_pa_t_kernel(tc, x, Wq, bq, Wk, bk, out_0, out_1)
         grouped_of = {}
         for n in range(2, 2 * UNITS):
             z, u = divmod(n, UNITS)
-            grouped_of[n] = group_weight(nc.gpsimd, z, u)
+            grouped_of[n] = group_weight(nc.scalar if n in GROUPED_ON_SCALAR else nc.gpsimd, z, u)
 
         for k in range(N_PAIRS + TURN_LAG):
             if k + 1 < N_PAIRS:

@@ -33,9 +33,9 @@ FREQ_STEP = ROPE_BASE ** (-2.0 / D_OUT)
 ROUND_MAGIC = 12582912.0
 
 FIRST_SHARED_QUAD = 2
-SHARED_QUADS = N_PAIRS // PARITIES - 1
+LAST_QUAD = N_PAIRS // PARITIES - 1
 ADDED, MULTIPLIED = 0, 1
-MULTIPLIED_QUADS = (0, 3)
+MULTIPLIED_QUADS = (0, 2, 3)
 ADDED_QUADS = (0, 1, 2)
 QUANTISE_STEP = 4
 TURN_LAG = 3
@@ -69,9 +69,16 @@ def tile_ropemultiheadattention_pa_t_kernel(tc, x, Wq, bq, Wk, bk, out_0, out_1)
                 in_=x[first : first + count, t * P : (t + 1) * P, :].rearrange("b p k -> p b k"),
             )
 
-        def load_weight(w, label):
+        def load_weight(w, label, groups):
             raw = const.tile([P, PACK, D_OUT], BF16, name="raw_" + label)
-            nc.sync.dma_start(out=raw[:], in_=w.rearrange("(q t) c -> q t c", t=PACK))
+            rows = w.rearrange("(q t) c -> q t c", t=PACK)
+            if groups == 1:
+                nc.sync.dma_start(out=raw[:], in_=rows)
+            else:
+                for g in range(groups):
+                    for h in range(HALVES):
+                        c = slice((h * groups + g) * 2 * P, (h * groups + g + 1) * 2 * P)
+                        nc.sync.dma_start(out=raw[:, :, c], in_=rows[:, :, c])
             return raw
 
         bias_rows = const.tile([P, PARITIES * P], BF16, name="bias_rows")
@@ -80,8 +87,8 @@ def tile_ropemultiheadattention_pa_t_kernel(tc, x, Wq, bq, Wk, bk, out_0, out_1)
         load_x(0, 2, 2)
         nc.sync.dma_start(out=bias_rows[0:N_FREQ, :], in_=bq.rearrange("(r c) -> r c", r=N_FREQ))
         nc.sync.dma_start(out=bias_rows[N_FREQ : 2 * N_FREQ, :], in_=bk.rearrange("(r c) -> r c", r=N_FREQ))
-        raw = [load_weight(Wq, "q")]
-        raw.append(load_weight(Wk, "k"))
+        raw = [load_weight(Wq, "q", GROUPS)]
+        raw.append(load_weight(Wk, "k", 1))
         for t in range(1, N_BLOCKS):
             load_x(t, 0, BATCH)
 
@@ -301,7 +308,7 @@ def tile_ropemultiheadattention_pa_t_kernel(tc, x, Wq, bq, Wk, bk, out_0, out_1)
             elif part == 7:
                 sines(t, 1, (SIN, COS + 1))
 
-        banks_of, products_of, stage_of = {}, {}, {}
+        banks_of, products_of, sums_of, stage_of = {}, {}, {}, {}
 
         def where(k):
             t, rest = divmod(k, PAIRS_PER_BLOCK)
@@ -330,7 +337,7 @@ def tile_ropemultiheadattention_pa_t_kernel(tc, x, Wq, bq, Wk, bk, out_0, out_1)
             banks_of[k] = banks
 
         def shared(k):
-            return FIRST_SHARED_QUAD <= k // PARITIES < SHARED_QUADS
+            return FIRST_SHARED_QUAD <= k // PARITIES < LAST_QUAD
 
         def quad_of_block(k):
             return k % PAIRS_PER_BLOCK // PARITIES
@@ -385,41 +392,58 @@ def tile_ropemultiheadattention_pa_t_kernel(tc, x, Wq, bq, Wk, bk, out_0, out_1)
                 own, other = products_of[k][:, COS:KINDS, :], products_of[k][:, MINUS_SIN:COS, :]
                 nc.gpsimd.tensor_tensor(out=own, in0=own, in1=other, op=ALU.add)
 
-        def sum_and_turn(k):
-            first_pair = k - k % 2
-            t, z, g, parity = where(first_pair)
+        def turn_pair(k, b):
+            quad, e = divmod(k, PARITIES)
+            if (quad, b) not in sums_of:
+                spare = quad == LAST_QUAD and b >= BATCH // 2
+                if spare:
+                    sums_of[(quad, b)] = mx_psum.tile([P, HALVES, PARITIES, P], F32, name="bank", tag="bank")
+                else:
+                    sums_of[(quad, b)] = sum_psum.tile([P, HALVES, PARITIES, P], F32, name="sums", tag="sums")
+            sums = sums_of[(quad, b)]
+            tokens = slice(b * P, (b + 1) * P)
+            whole = added_on_gpsimd(k)
+            for h in range(HALVES):
+                nc.tensor.matmul(
+                    out=sums[:, h, e, :], lhsT=products_of[k][:, COS + h, tokens], rhs=ident[:],
+                    is_transpose=True, start=True, stop=whole,
+                )
+                if not whole:
+                    nc.tensor.matmul(
+                        out=sums[:, h, e, :], lhsT=products_of[k][:, MINUS_SIN + h, tokens], rhs=ident[:],
+                        is_transpose=True, start=False, stop=True,
+                    )
+
+        def bring_out(quad, b):
+            t, z, g, parity = where(PARITIES * quad)
             if (t, z) not in stage_of:
                 stage_of[(t, z)] = stage_pool.tile([P, BATCH, D_OUT], F32, name="stage", tag="stage")
             stage = stage_of[(t, z)]
-            last_stage = (t, z) == (N_BLOCKS - 1, 1)
-            for b in (2 * (k % 2), 2 * (k % 2) + 1):
-                tokens = slice(b * P, (b + 1) * P)
-                sums = sum_psum.tile([P, HALVES, PARITIES, P], F32, name="sums", tag="sums")
-                for e in range(PARITIES):
-                    products = products_of[first_pair + e]
-                    whole = added_on_gpsimd(first_pair + e)
-                    for h in range(HALVES):
-                        nc.tensor.matmul(
-                            out=sums[:, h, e, :], lhsT=products[:, COS + h, tokens], rhs=ident[:],
-                            is_transpose=True, start=True, stop=whole,
-                        )
-                        if not whole:
-                            nc.tensor.matmul(
-                                out=sums[:, h, e, :], lhsT=products[:, MINUS_SIN + h, tokens], rhs=ident[:],
-                                is_transpose=True, start=False, stop=True,
-                            )
-                by_group = stage[:, b, :].rearrange("p (h g c) -> p g h c", h=HALVES, g=GROUPS)[:, g]
-                nc.scalar.copy(
-                    out=by_group.rearrange("p h (c e) -> p h c e", e=PARITIES),
-                    in_=sums[:].rearrange("p h e c -> p h c e"),
+            by_group = stage[:, b, :].rearrange("p (h g c) -> p g h c", h=HALVES, g=GROUPS)[:, g]
+            nc.scalar.copy(
+                out=by_group.rearrange("p h (c e) -> p h c e", e=PARITIES),
+                in_=sums_of[(quad, b)][:].rearrange("p h e c -> p h c e"),
+            )
+            rows = outs[z][b, t * P : (t + 1) * P, :]
+            if (t, z) == (N_BLOCKS - 1, 1):
+                nc.sync.dma_start(
+                    out=rows.rearrange("p (h g c) -> p g h c", h=HALVES, g=GROUPS)[:, g], in_=by_group
                 )
-                rows = outs[z][b, t * P : (t + 1) * P, :]
-                if last_stage:
-                    nc.sync.dma_start(
-                        out=rows.rearrange("p (h g c) -> p g h c", h=HALVES, g=GROUPS)[:, g], in_=by_group
-                    )
-                elif g == GROUPS - 1:
-                    nc.sync.dma_start(out=rows, in_=stage[:, b, :])
+            elif g == GROUPS - 1:
+                nc.sync.dma_start(out=rows, in_=stage[:, b, :])
+
+        def turn_half(k):
+            quad, part = divmod(k, PARITIES)
+            if quad == LAST_QUAD:
+                for b in range(BATCH):
+                    turn_pair(k, b)
+                    if part == 1:
+                        bring_out(quad, b)
+            else:
+                for b in (2 * part, 2 * part + 1):
+                    turn_pair(PARITIES * quad, b)
+                    turn_pair(PARITIES * quad + 1, b)
+                    bring_out(quad, b)
 
         turn_x(0, 0)
         turn_x(0, 2)
@@ -429,11 +453,11 @@ def tile_ropemultiheadattention_pa_t_kernel(tc, x, Wq, bq, Wk, bk, out_0, out_1)
         for g in range(GROUPS):
             folds(0, g)
             sines(0, g, range(KINDS))
+        quantise_x(0)
         weights = {}
         weights[(0, 0)] = quantise_weight(0, 0, group_weight(nc.vector, 0, 0))
         bias = const.tile([P, PARITIES, 2 * N_FREQ], F32, name="bias")
         nc.vector.tensor_copy(out=bias[:], in_=bias_cols[:, :, 0 : 2 * N_FREQ])
-        quantise_x(0)
         project(0)
         weights[(0, 1)] = quantise_weight(0, 1, group_weight(nc.vector, 0, 1))
         grouped_of = {}
@@ -452,7 +476,7 @@ def tile_ropemultiheadattention_pa_t_kernel(tc, x, Wq, bq, Wk, bk, out_0, out_1)
                 rotate(k)
                 add_share(k)
             if k >= TURN_LAG:
-                sum_and_turn(k - TURN_LAG)
+                turn_half(k - TURN_LAG)
             t, part = divmod(k, PAIRS_PER_BLOCK)
             if t + 1 < N_BLOCKS:
                 prepare(t + 1, part)

@@ -35,12 +35,12 @@ ROUND_MAGIC = 12582912.0
 FIRST_SHARED_QUAD = 2
 LAST_QUAD = N_PAIRS // PARITIES - 1
 ADDED, MULTIPLIED = 0, 1
-MULTIPLIED_QUADS = (0, 2, 3)
+MULTIPLIED_QUADS = (0, 3)
 ADDED_QUADS = (0, 1, 2)
 QUANTISE_STEP = 4
 TURN_LAG = 3
 
-GROUPED_ON_SCALAR = (2, 3)
+GROUPED_ON_SCALAR = (1, 2, 3)
 
 FLOPS = 2 * BATCH * SEQ * D_IN * 2 * D_OUT
 
@@ -58,7 +58,8 @@ def tile_ropemultiheadattention_pa_t_kernel(tc, x, Wq, bq, Wk, bk, out_0, out_1)
         prod_pool = ctx.enter_context(tc.tile_pool(name="prod", bufs=8))
         value_pool = ctx.enter_context(tc.tile_pool(name="value", bufs=2))
         stage_pool = ctx.enter_context(tc.tile_pool(name="stage", bufs=3))
-        mx_psum = ctx.enter_context(tc.psum_pool(name="mx_psum", bufs=5))
+        mx_psum = ctx.enter_context(tc.psum_pool(name="mx_psum", bufs=4))
+        bias_psum = ctx.enter_context(tc.psum_pool(name="bias_psum", bufs=1))
         sum_psum = ctx.enter_context(tc.psum_pool(name="sum_psum", bufs=3))
 
         xin = const.tile([P, N_BLOCKS, BATCH, D_IN], BF16, name="xin")
@@ -69,26 +70,30 @@ def tile_ropemultiheadattention_pa_t_kernel(tc, x, Wq, bq, Wk, bk, out_0, out_1)
                 in_=x[first : first + count, t * P : (t + 1) * P, :].rearrange("b p k -> p b k"),
             )
 
-        def load_weight(w, label, groups):
-            raw = const.tile([P, PACK, D_OUT], BF16, name="raw_" + label)
+        def raw_tile(label):
+            return const.tile([P, PACK, D_OUT], BF16, name="raw_" + label)
+
+        def load_weight(z, w, groups):
             rows = w.rearrange("(q t) c -> q t c", t=PACK)
-            if groups == 1:
-                nc.sync.dma_start(out=raw[:], in_=rows)
-            else:
-                for g in range(groups):
-                    for h in range(HALVES):
-                        c = slice((h * groups + g) * 2 * P, (h * groups + g + 1) * 2 * P)
-                        nc.sync.dma_start(out=raw[:, :, c], in_=rows[:, :, c])
-            return raw
+            if groups is None:
+                nc.sync.dma_start(out=raw[z][:], in_=rows)
+                return
+            for g in groups:
+                for h in range(HALVES):
+                    first = (h * GROUPS + g) * PARITIES * P
+                    columns = slice(first, first + PARITIES * P)
+                    nc.sync.dma_start(out=raw[z][:, :, columns], in_=rows[:, :, columns])
 
         bias_rows = const.tile([P, PARITIES * P], BF16, name="bias_rows")
         nc.gpsimd.memset(bias_rows[:], 0.0)
         load_x(0, 0, 2)
         load_x(0, 2, 2)
+        raw = [raw_tile("q"), raw_tile("k")]
+        load_weight(0, Wq, range(0, 1))
         nc.sync.dma_start(out=bias_rows[0:N_FREQ, :], in_=bq.rearrange("(r c) -> r c", r=N_FREQ))
         nc.sync.dma_start(out=bias_rows[N_FREQ : 2 * N_FREQ, :], in_=bk.rearrange("(r c) -> r c", r=N_FREQ))
-        raw = [load_weight(Wq, "q", GROUPS)]
-        raw.append(load_weight(Wk, "k", 1))
+        load_weight(0, Wq, range(1, GROUPS))
+        load_weight(1, Wk, None)
         for t in range(1, N_BLOCKS):
             load_x(t, 0, BATCH)
 
@@ -161,8 +166,6 @@ def tile_ropemultiheadattention_pa_t_kernel(tc, x, Wq, bq, Wk, bk, out_0, out_1)
         block_whole = const.tile(block_shape, F32, name="block_whole")
         block_frac = const.tile(block_shape, F32, name="block_frac")
         nearest_whole_removed(nc.gpsimd, block_frac[:], block_angle[:], block_whole[:])
-        bias_rows_f32 = const.tile([P, PARITIES * P], F32, name="bias_rows_f32")
-        nc.gpsimd.tensor_copy(out=bias_rows_f32[:], in_=bias_rows[:])
         column_shape = [P, N_BLOCKS, KINDS * GROUPS]
 
         def column_tile(name):
@@ -361,16 +364,16 @@ def tile_ropemultiheadattention_pa_t_kernel(tc, x, Wq, bq, Wk, bk, out_0, out_1)
         def twice(tile):
             return tile[:].rearrange("f (b p) -> f b p", b=BATCH).unsqueeze(1).to_broadcast(two_tables)
 
-        def bias_col(k, h):
+        def bias_col(columns, k, h):
             t, z, g, e = where(k)
             row = N_FREQ * z + GROUPS * h + g
-            return bias[:, e, row : row + 1]
+            return columns[:, e, row : row + 1]
 
         def multiply_share(k):
             for h in range(HALVES):
                 if multiplied_on_gpsimd(k, h):
                     value = value_pool.tile([P, TOKENS], F32, name="value", tag="value")
-                    nc.scalar.activation(out=value[:], in_=banks_of[k][h][:], func=ACT.Identity, bias=bias_col(k, h))
+                    nc.scalar.activation(out=value[:], in_=banks_of[k][h][:], func=ACT.Identity, bias=bias_col(bias, k, h))
                     out, tables = factors(k, h)
                     nc.gpsimd.tensor_tensor(out=out, in0=twice(value), in1=tables, op=ALU.mult)
 
@@ -381,11 +384,15 @@ def tile_ropemultiheadattention_pa_t_kernel(tc, x, Wq, bq, Wk, bk, out_0, out_1)
                     for n in range(2):
                         nc.vector.scalar_tensor_tensor(
                             out=out[:, n], in0=banks_of[k][h][:].rearrange("f (b p) -> f b p", b=BATCH),
-                            scalar=bias_col(k, h), in1=tables[:, n], op0=ALU.add, op1=ALU.mult,
+                            scalar=bias_col(bias_cols, k, h), in1=tables[:, n], op0=ALU.add, op1=ALU.mult,
                         )
                 t, part = divmod(k, PAIRS_PER_BLOCK)
-                if h == 0 and part == QUANTISE_STEP and t + 1 < N_BLOCKS:
-                    quantise_x(t + 1)
+                if h == 0:
+                    if part == QUANTISE_STEP and t + 1 < N_BLOCKS:
+                        quantise_x(t + 1)
+                    for n in (1, 2) if k == 0 else (k + 2,):
+                        if n in grouped_of:
+                            weights[divmod(n, UNITS)] = quantise_weight(*divmod(n, UNITS), grouped_of[n])
 
         def add_share(k):
             if added_on_gpsimd(k):
@@ -419,13 +426,15 @@ def tile_ropemultiheadattention_pa_t_kernel(tc, x, Wq, bq, Wk, bk, out_0, out_1)
             if (t, z) not in stage_of:
                 stage_of[(t, z)] = stage_pool.tile([P, BATCH, D_OUT], F32, name="stage", tag="stage")
             stage = stage_of[(t, z)]
-            by_group = stage[:, b, :].rearrange("p (h g c) -> p g h c", h=HALVES, g=GROUPS)[:, g]
+            last_stage = (t, z) == (N_BLOCKS - 1, 1)
+            order = "p (g h c) -> p g h c" if last_stage else "p (h g c) -> p g h c"
+            by_group = stage[:, b, :].rearrange(order, h=HALVES, g=GROUPS)[:, g]
             nc.scalar.copy(
                 out=by_group.rearrange("p h (c e) -> p h c e", e=PARITIES),
                 in_=sums_of[(quad, b)][:].rearrange("p h e c -> p h c e"),
             )
             rows = outs[z][b, t * P : (t + 1) * P, :]
-            if (t, z) == (N_BLOCKS - 1, 1):
+            if last_stage:
                 nc.sync.dma_start(
                     out=rows.rearrange("p (h g c) -> p g h c", h=HALVES, g=GROUPS)[:, g], in_=by_group
                 )
@@ -447,36 +456,41 @@ def tile_ropemultiheadattention_pa_t_kernel(tc, x, Wq, bq, Wk, bk, out_0, out_1)
 
         turn_x(0, 0)
         turn_x(0, 2)
-        bias_cols = sum_psum.tile([P, PARITIES, P], F32, name="bias_cols", tag="sums")
+        folds(0, 0)
+        sines(0, 0, range(KINDS))
+        bias_rows_f32 = const.tile([P, PARITIES * P], F32, name="bias_rows_f32")
+        nc.scalar.copy(out=bias_rows_f32[:], in_=bias_rows[:])
+        bias_cols = bias_psum.tile([P, PARITIES, P], F32, name="bias_cols", tag="bias_cols")
         for e in range(PARITIES):
             nc.tensor.transpose(out=bias_cols[:, e, :], in_=bias_rows_f32[:, e : 2 * P : 2], identity=ident[:])
-        for g in range(GROUPS):
-            folds(0, g)
-            sines(0, g, range(KINDS))
         quantise_x(0)
         weights = {}
         weights[(0, 0)] = quantise_weight(0, 0, group_weight(nc.vector, 0, 0))
         bias = const.tile([P, PARITIES, 2 * N_FREQ], F32, name="bias")
         nc.vector.tensor_copy(out=bias[:], in_=bias_cols[:, :, 0 : 2 * N_FREQ])
         project(0)
-        weights[(0, 1)] = quantise_weight(0, 1, group_weight(nc.vector, 0, 1))
         grouped_of = {}
-        for n in range(2, 2 * UNITS):
+        for n in range(1, 2 * UNITS):
             z, u = divmod(n, UNITS)
             grouped_of[n] = group_weight(nc.scalar if n in GROUPED_ON_SCALAR else nc.gpsimd, z, u)
+        folds(0, 1)
+        sines(0, 1, range(KINDS))
 
+        turned = 0
         for k in range(N_PAIRS + TURN_LAG):
-            if k + 1 < N_PAIRS:
+            if 0 < k < N_PAIRS - 1:
                 project(k + 1)
-            if k + 2 in grouped_of:
-                weights[divmod(k + 2, UNITS)] = quantise_weight(*divmod(k + 2, UNITS), grouped_of[k + 2])
             if k + 1 < N_PAIRS:
                 multiply_share(k + 1)
             if k < N_PAIRS:
                 rotate(k)
+                if k == 0:
+                    project(1)
                 add_share(k)
-            if k >= TURN_LAG:
-                turn_half(k - TURN_LAG)
+            lag = TURN_LAG if shared(turned) else TURN_LAG - 1
+            if turned < N_PAIRS and turned + lag <= k:
+                turn_half(turned)
+                turned += 1
             t, part = divmod(k, PAIRS_PER_BLOCK)
             if t + 1 < N_BLOCKS:
                 prepare(t + 1, part)

@@ -58,8 +58,7 @@ def tile_ropemultiheadattention_pa_t_kernel(tc, x, Wq, bq, Wk, bk, out_0, out_1)
         prod_pool = ctx.enter_context(tc.tile_pool(name="prod", bufs=8))
         value_pool = ctx.enter_context(tc.tile_pool(name="value", bufs=2))
         stage_pool = ctx.enter_context(tc.tile_pool(name="stage", bufs=3))
-        mx_psum = ctx.enter_context(tc.psum_pool(name="mx_psum", bufs=4))
-        bias_psum = ctx.enter_context(tc.psum_pool(name="bias_psum", bufs=1))
+        mx_psum = ctx.enter_context(tc.psum_pool(name="mx_psum", bufs=5))
         sum_psum = ctx.enter_context(tc.psum_pool(name="sum_psum", bufs=3))
 
         xin = const.tile([P, N_BLOCKS, BATCH, D_IN], BF16, name="xin")
@@ -384,12 +383,12 @@ def tile_ropemultiheadattention_pa_t_kernel(tc, x, Wq, bq, Wk, bk, out_0, out_1)
                     for n in range(2):
                         nc.vector.scalar_tensor_tensor(
                             out=out[:, n], in0=banks_of[k][h][:].rearrange("f (b p) -> f b p", b=BATCH),
-                            scalar=bias_col(bias_cols, k, h), in1=tables[:, n], op0=ALU.add, op1=ALU.mult,
+                            scalar=bias_col(bias, k, h), in1=tables[:, n], op0=ALU.add, op1=ALU.mult,
                         )
                 t, part = divmod(k, PAIRS_PER_BLOCK)
+                if h == 1 and part == QUANTISE_STEP and t + 1 < N_BLOCKS:
+                    quantise_x(t + 1)
                 if h == 0:
-                    if part == QUANTISE_STEP and t + 1 < N_BLOCKS:
-                        quantise_x(t + 1)
                     for n in (1, 2) if k == 0 else (k + 2,):
                         if n in grouped_of:
                             weights[divmod(n, UNITS)] = quantise_weight(*divmod(n, UNITS), grouped_of[n])
@@ -460,7 +459,7 @@ def tile_ropemultiheadattention_pa_t_kernel(tc, x, Wq, bq, Wk, bk, out_0, out_1)
         sines(0, 0, range(KINDS))
         bias_rows_f32 = const.tile([P, PARITIES * P], F32, name="bias_rows_f32")
         nc.scalar.copy(out=bias_rows_f32[:], in_=bias_rows[:])
-        bias_cols = bias_psum.tile([P, PARITIES, P], F32, name="bias_cols", tag="bias_cols")
+        bias_cols = sum_psum.tile([P, PARITIES, P], F32, name="bias_cols", tag="sums")
         for e in range(PARITIES):
             nc.tensor.transpose(out=bias_cols[:, e, :], in_=bias_rows_f32[:, e : 2 * P : 2], identity=ident[:])
         quantise_x(0)

from contextlib import ExitStack

import concourse.masks as masks
import concourse.mybir as mybir

F32 = mybir.dt.float32
BF16 = mybir.dt.bfloat16
U32 = mybir.dt.uint32
U8 = mybir.dt.uint8
FP8X4 = mybir.dt.float8_e4m3fn_x4
ALU = mybir.AluOpType
ACT = mybir.ActivationFunctionType

P = 128
PACK = 4
BATCH, SEQ, D_IN, D_OUT = 4, 1024, 512, 1024
ROPE_BASE = 10000.0
PI = 3.141592653589793
assert D_IN == P * PACK

N_BLOCKS = SEQ // P
TOKENS = BATCH * P
HALVES = 2
GROUPS = 2
PARITIES = 2
N_FREQ = HALVES * GROUPS
UNITS = GROUPS * PARITIES
PAIRS_PER_BLOCK = 2 * UNITS
N_PAIRS = N_BLOCKS * PAIRS_PER_BLOCK
MINUS_SIN, SIN, COS, KINDS = 0, 1, 2, 4

FREQ_STEP = ROPE_BASE ** (-2.0 / D_OUT)
ROUND_MAGIC = 12582912.0

FIRST_SHARED_QUAD = 2
LAST_QUAD = N_PAIRS // PARITIES - 1
ADDED, MULTIPLIED = 0, 1
MULTIPLIED_QUADS = (0, 3)
ADDED_QUADS = (0, 1, 2)
QUANTISE_STEP = 4
TURN_LAG = 3

GROUPED_ON_SCALAR = (1, 2, 3)

FLOPS = 2 * BATCH * SEQ * D_IN * 2 * D_OUT


def tile_ropemultiheadattention_pa_t_kernel(tc, x, Wq, bq, Wk, bk, out_0, out_1):
    nc = tc.nc
    outs = (out_0, out_1)
    with ExitStack() as ctx:
        ctx.enter_context(tc.manual_schedule())
        const = ctx.enter_context(tc.tile_pool(name="const", bufs=1))
        xq_pool = ctx.enter_context(tc.tile_pool(name="xq", bufs=2))
        xw_pool = ctx.enter_context(tc.tile_pool(name="xw", bufs=2))
        fold_pool = ctx.enter_context(tc.tile_pool(name="fold", bufs=2))
        trig_pool = ctx.enter_context(tc.tile_pool(name="trig", bufs=2))
        prod_pool = ctx.enter_context(tc.tile_pool(name="prod", bufs=8))
        value_pool = ctx.enter_context(tc.tile_pool(name="value", bufs=2))
        stage_pool = ctx.enter_context(tc.tile_pool(name="stage", bufs=3))
        mx_psum = ctx.enter_context(tc.psum_pool(name="mx_psum", bufs=5))
        sum_psum = ctx.enter_context(tc.psum_pool(name="sum_psum", bufs=3))

        xin = const.tile([P, N_BLOCKS, BATCH, D_IN], BF16, name="xin")

        def load_x(t, first, count):
            nc.sync.dma_start(
                out=xin[:, t, first : first + count, :],
                in_=x[first : first + count, t * P : (t + 1) * P, :].rearrange("b p k -> p b k"),
            )

        def raw_tile(label):
            return const.tile([P, PACK, D_OUT], BF16, name="raw_" + label)

        def load_weight(z, w, groups):
            rows = w.rearrange("(q t) c -> q t c", t=PACK)
            if groups is None:
                nc.sync.dma_start(out=raw[z][:], in_=rows)
                return
            for g in groups:
                for h in range(HALVES):
                    first = (h * GROUPS + g) * PARITIES * P
                    columns = slice(first, first + PARITIES * P)
                    nc.sync.dma_start(out=raw[z][:, :, columns], in_=rows[:, :, columns])

        bias_rows = const.tile([P, PARITIES * P], BF16, name="bias_rows")
        nc.gpsimd.memset(bias_rows[:], 0.0)
        load_x(0, 0, 2)
        load_x(0, 2, 2)
        raw = [raw_tile("q"), raw_tile("k")]
        load_weight(0, Wq, range(0, 1))
        nc.sync.dma_start(out=bias_rows[0:N_FREQ, :], in_=bq.rearrange("(r c) -> r c", r=N_FREQ))
        nc.sync.dma_start(out=bias_rows[N_FREQ : 2 * N_FREQ, :], in_=bk.rearrange("(r c) -> r c", r=N_FREQ))
        load_weight(0, Wq, range(1, GROUPS))
        load_weight(1, Wk, None)
        for t in range(1, N_BLOCKS):
            load_x(t, 0, BATCH)

        ident = const.tile([P, P], F32, name="ident")
        masks.make_identity(nc, ident[:])
        pos = const.tile([P, P], F32, name="pos")
        nc.gpsimd.iota(
            pos[:], pattern=[[1, P]], base=0, channel_multiplier=0, allow_small_or_imprecise_dtypes=True
        )

        minus_half = const.tile([P, 1], F32, name="minus_half")
        nc.vector.memset(minus_half[:], -0.5)
        minus_quarter = const.tile([P, 1], F32, name="minus_quarter")
        nc.vector.memset(minus_quarter[:], -0.25)
        half_pi = const.tile([P, 1], F32, name="half_pi")
        nc.vector.tensor_scalar_mul(out=half_pi[:], in0=minus_half[:], scalar1=-PI)
        minus_half_pi = const.tile([P, 1], F32, name="minus_half_pi")
        nc.vector.tensor_scalar_mul(out=minus_half_pi[:], in0=minus_half[:], scalar1=PI)
        warm = const.tile([P, 1], F32, name="warm")
        nc.scalar.activation(out=warm[:], in_=minus_half[:], func=ACT.Sin)

        step_row = const.tile([P, P], F32, name="step_row")
        nc.vector.memset(step_row[:, 0:1], 1.0)
        w = 1
        while w < P:
            nc.vector.tensor_scalar_mul(
                out=step_row[:, w : 2 * w], in0=step_row[:, 0:w], scalar1=FREQ_STEP**w
            )
            w *= 2

        step_col = sum_psum.tile([P, P], F32, name="step_col", tag="sums")
        nc.tensor.transpose(out=step_col[:], in_=step_row[:], identity=ident[:])
        turns = const.tile([P, N_FREQ], F32, name="turns")
        for f in range(N_FREQ):
            nc.vector.tensor_scalar_mul(
                out=turns[:, f : f + 1], in0=step_col[:, 0:1], scalar1=FREQ_STEP ** (f * P) / (2.0 * PI)
            )

        def nearest_whole_removed(engine, out, value, scratch):
            engine.tensor_scalar(
                out=scratch, in0=value, scalar1=ROUND_MAGIC, scalar2=ROUND_MAGIC,
                op0=ALU.add, op1=ALU.subtract,
            )
            engine.tensor_tensor(out=out, in0=value, in1=scratch, op=ALU.subtract)

        table_shape = [P, N_FREQ, P]
        angle0 = const.tile(table_shape, F32, name="angle0")
        nc.vector.tensor_tensor(
            out=angle0[:],
            in0=pos[:].unsqueeze(1).to_broadcast(table_shape),
            in1=turns[:].unsqueeze(2).to_broadcast(table_shape),
            op=ALU.mult,
        )
        whole0 = const.tile(table_shape, F32, name="whole0")
        frac0 = const.tile(table_shape, F32, name="frac0")
        nearest_whole_removed(nc.vector, frac0[:], angle0[:], whole0[:])

        block_shape = [P, N_BLOCKS, N_FREQ]
        block_turns = const.tile([P, N_FREQ], F32, name="block_turns")
        nc.gpsimd.tensor_scalar(
            out=block_turns[:], in0=turns[:], scalar1=float(P), scalar2=0.0, op0=ALU.mult, op1=ALU.add
        )
        block_angle = const.tile(block_shape, F32, name="block_angle")
        nc.gpsimd.tensor_tensor(
            out=block_angle[:],
            in0=pos[:, 0:N_BLOCKS].unsqueeze(2).to_broadcast(block_shape),
            in1=block_turns[:].unsqueeze(1).to_broadcast(block_shape),
            op=ALU.mult,
        )
        block_whole = const.tile(block_shape, F32, name="block_whole")
        block_frac = const.tile(block_shape, F32, name="block_frac")
        nearest_whole_removed(nc.gpsimd, block_frac[:], block_angle[:], block_whole[:])
        column_shape = [P, N_BLOCKS, KINDS * GROUPS]

        def column_tile(name):
            return const.tile(column_shape, F32, name=name)

        def of_kind(tile, kind, count=1):
            return tile[:, :, kind * GROUPS : (kind + count) * GROUPS]

        def affine(out, value, factor, addend):
            nc.gpsimd.tensor_scalar(
                out=out, in0=value, scalar1=factor, scalar2=addend, op0=ALU.mult, op1=ALU.add
            )

        half_turns = column_tile("half_turns")
        lower, upper = block_frac[:, :, 0:GROUPS], block_frac[:, :, GROUPS:N_FREQ]
        affine(of_kind(half_turns, MINUS_SIN), lower, 2.0, -0.5)
        affine(of_kind(half_turns, SIN), upper, 2.0, 0.0)
        affine(of_kind(half_turns, COS), lower, 2.0, 0.0)
        affine(of_kind(half_turns, COS + 1), upper, 2.0, 0.5)
        half_whole = column_tile("half_whole")
        half_frac = column_tile("half_frac")
        nearest_whole_removed(nc.gpsimd, half_frac[:], half_turns[:], half_whole[:])
        pairs = column_tile("pairs")
        affine(pairs[:], half_whole[:], 0.5, 0.0)
        pairs_whole = column_tile("pairs_whole")
        pairs_frac = column_tile("pairs_frac")
        nearest_whole_removed(nc.gpsimd, pairs_frac[:], pairs[:], pairs_whole[:])
        sign = column_tile("sign")
        nc.gpsimd.tensor_tensor(out=sign[:], in0=pairs_frac[:], in1=pairs_frac[:], op=ALU.mult)
        affine(sign[:], sign[:], -8.0, 1.0)
        turn_shift, sine_scale, sine_bias = column_tile("turn_shift"), column_tile("sine_scale"), column_tile("sine_bias")
        affine(turn_shift[:], half_frac[:], 0.5, 0.0)
        affine(sine_scale[:], sign[:], 2.0 * PI, 0.0)
        affine(of_kind(sine_scale, COS), of_kind(sign, COS), -2.0 * PI, 0.0)
        nc.gpsimd.tensor_tensor(out=sine_bias[:], in0=sine_scale[:], in1=turn_shift[:], op=ALU.mult)
        for kind in (MINUS_SIN, COS):
            affine(of_kind(sine_bias, kind), of_kind(sine_scale, kind), -0.25, 0.0)

        def group_weight(engine, z, u):
            g, e = divmod(u, PARITIES)
            grouped = const.tile([P, HALVES, P, PACK], BF16, name="w_grouped%d%d" % (z, u), align_bytes=64)
            for h in range(HALVES):
                columns = raw[z][:].rearrange(
                    "q t (h g p e) -> q h g e p t", h=HALVES, g=GROUPS, e=PARITIES
                )[:, h, g, e]
                if engine is nc.vector:
                    nc.vector.tensor_copy(
                        out=grouped[:, h].rearrange("q (c i) t -> q c t i", i=4),
                        in_=columns.rearrange("q (c i) t -> q c t i", i=4),
                    )
                elif engine is nc.scalar:
                    engine.copy(out=grouped[:, h], in_=columns)
                else:
                    engine.tensor_scalar(
                        out=grouped[:, h], in0=columns, scalar1=1.0, scalar2=0.0, op0=ALU.mult, op1=ALU.add
                    )
            return grouped

        def quantise_weight(z, u, grouped):
            codes = const.tile([P, HALVES * P], U32, name="w_codes%d%d" % (z, u), align_bytes=64)
            scales = const.tile([P, HALVES * P], U8, name="w_scales%d%d" % (z, u), align_bytes=64)
            nc.vector.quantize_mx(
                out=codes[:].bitcast(FP8X4), scales=scales[:], in_=grouped[:].rearrange("q h p t -> q (h p t)")
            )
            return codes, scales

        fold_of, trig_of, x_words_of, x_grouped_of, x_quantised_of = {}, {}, {}, {}, {}

        def folds(t, g):
            fold_of[(t, g)] = fold_pool.tile([P, 2, P], F32, name="fold", tag="fold")
            for n, kind in enumerate((MINUS_SIN, COS)):
                column = kind * GROUPS + g
                shift = turn_shift[:, t, column : column + 1] if t else (minus_quarter[:, 0:1], 0.0)[n]
                nc.scalar.activation(out=fold_of[(t, g)][:, n, :], in_=frac0[:, g, :], func=ACT.Abs, bias=shift)

        def sines(t, g, kinds):
            if t not in trig_of:
                trig_of[t] = trig_pool.tile([P, GROUPS, KINDS, P], F32, name="trig", tag="trig")
            for kind in kinds:
                column = kind * GROUPS + g
                if t:
                    scale, bias_here = sine_scale[:, t, column : column + 1], sine_bias[:, t, column : column + 1]
                else:
                    scale = -2.0 * PI if kind == COS else 2.0 * PI
                    bias_here = {MINUS_SIN: minus_half_pi[:, 0:1], SIN: 0.0}.get(kind, half_pi[:, 0:1])
                source = frac0[:, g + GROUPS, :] if kind % 2 else fold_of[(t, g)][:, kind // 2, :]
                nc.scalar.activation(
                    out=trig_of[t][:, g, kind], in_=source, func=ACT.Sin, scale=scale, bias=bias_here
                )

        def separate_words(t, first):
            if first == 0:
                x_words_of[t] = xw_pool.tile([P, BATCH, 2, P], F32, name="x_words", tag="x_words")
            two = slice(first, first + 2)
            nc.scalar.copy(
                out=x_words_of[t][:, two],
                in_=xin[:, t, two, :].rearrange("p b k -> p (b k)").bitcast(F32).rearrange("p (b w u) -> p b u w", b=2, u=2),
            )

        def turn_x(t, first):
            if first == 0:
                x_grouped_of[t] = xq_pool.tile([P, TOKENS, 2], F32, name="x_grouped", tag="x_grouped", align_bytes=64)
            xt = sum_psum.tile([P, 2, 2, P], F32, name="xt", tag="sums")
            for b in range(2):
                for u in range(2):
                    if t == 0:
                        words = xin[:, t, first + b, :].bitcast(F32)[:, u : 2 * P : 2]
                    else:
                        words = x_words_of[t][:, first + b, u, :]
                    nc.tensor.transpose(out=xt[:, b, u, :], in_=words, identity=ident[:])
            nc.scalar.copy(
                out=x_grouped_of[t][:, first * P : (first + 2) * P, :].rearrange("w (b p) u -> w b p u", b=2),
                in_=xt[:].rearrange("w b u p -> w b p u"),
            )

        def quantise_x(t):
            codes = xq_pool.tile([P, TOKENS], U32, name="x_codes", tag="x_codes", align_bytes=64)
            scales = xq_pool.tile([P, TOKENS], U8, name="x_scales", tag="x_scales", align_bytes=64)
            nc.vector.quantize_mx(
                out=codes[:].bitcast(FP8X4),
                scales=scales[:],
                in_=x_grouped_of[t][:].rearrange("w c u -> w (c u)").bitcast(BF16),
            )
            x_quantised_of[t] = (codes, scales)

        def prepare(t, part):
            if part == 0:
                separate_words(t, 0)
            elif part == 1:
                separate_words(t, 2)
                turn_x(t, 0)
            elif part == 2:
                folds(t, 0)
                turn_x(t, 2)
            elif part == 3:
                sines(t, 0, (MINUS_SIN, COS))
            elif part == 4:
                sines(t, 0, (SIN, COS + 1))
            elif part == 5:
                folds(t, 1)
            elif part == 6:
                sines(t, 1, (MINUS_SIN, COS))
            elif part == 7:
                sines(t, 1, (SIN, COS + 1))

        banks_of, products_of, sums_of, stage_of = {}, {}, {}, {}

        def where(k):
            t, rest = divmod(k, PAIRS_PER_BLOCK)
            z, u = divmod(rest, UNITS)
            g, e = divmod(u, PARITIES)
            return t, z, g, e

        def project(k):
            t, z, g, e = where(k)
            x_codes, x_scales = x_quantised_of[t]
            w_codes, w_scales = weights[(z, PARITIES * g + e)]
            banks = []
            for h in range(HALVES):
                features = slice(h * P, (h + 1) * P)
                bank = mx_psum.tile([P, TOKENS], F32, name="bank", tag="bank")
                nc.tensor.matmul_mx(
                    out=bank[:],
                    lhsT=w_codes[:, features].bitcast(FP8X4),
                    lhsT_scale=w_scales[:, features],
                    rhs=x_codes[:].bitcast(FP8X4),
                    rhs_scale=x_scales[:],
                    start=True,
                    stop=True,
                )
                banks.append(bank)
            banks_of[k] = banks

        def shared(k):
            return FIRST_SHARED_QUAD <= k // PARITIES < LAST_QUAD

        def quad_of_block(k):
            return k % PAIRS_PER_BLOCK // PARITIES

        def multiplied_on_gpsimd(k, h):
            return shared(k) and quad_of_block(k) in MULTIPLIED_QUADS and (k % PARITIES, h) == (MULTIPLIED, 0)

        def added_on_gpsimd(k):
            return shared(k) and quad_of_block(k) in ADDED_QUADS and k % PARITIES == ADDED

        two_tables = [P, 2, BATCH, P]

        def factors(k, h):
            t, z, g, e = where(k)
            if k not in products_of:
                products_of[k] = prod_pool.tile([P, KINDS, TOKENS], F32, name="products", tag="products")
            kinds = slice(SIN, COS + 1) if h == 0 else slice(MINUS_SIN, KINDS, KINDS - 1)
            out = products_of[k][:, kinds, :].rearrange("f n (b p) -> f n b p", b=BATCH)
            return out, trig_of[t][:, g, kinds, :].unsqueeze(2).to_broadcast(two_tables)

        def twice(tile):
            return tile[:].rearrange("f (b p) -> f b p", b=BATCH).unsqueeze(1).to_broadcast(two_tables)

        def bias_col(columns, k, h):
            t, z, g, e = where(k)
            row = N_FREQ * z + GROUPS * h + g
            return columns[:, e, row : row + 1]

        def multiply_share(k):
            for h in range(HALVES):
                if multiplied_on_gpsimd(k, h):
                    value = value_pool.tile([P, TOKENS], F32, name="value", tag="value")
                    nc.scalar.activation(out=value[:], in_=banks_of[k][h][:], func=ACT.Identity, bias=bias_col(bias, k, h))
                    out, tables = factors(k, h)
                    nc.gpsimd.tensor_tensor(out=out, in0=twice(value), in1=tables, op=ALU.mult)

        def rotate(k):
            for h in range(HALVES):
                if not multiplied_on_gpsimd(k, h):
                    out, tables = factors(k, h)
                    for n in range(2):
                        nc.vector.scalar_tensor_tensor(
                            out=out[:, n], in0=banks_of[k][h][:].rearrange("f (b p) -> f b p", b=BATCH),
                            scalar=bias_col(bias, k, h), in1=tables[:, n], op0=ALU.add, op1=ALU.mult,
                        )
                t, part = divmod(k, PAIRS_PER_BLOCK)
                if h == 1 and part == QUANTISE_STEP and t + 1 < N_BLOCKS:
                    quantise_x(t + 1)
                if h == 0:
                    for n in (1, 2) if k == 0 else (k + 2,):
                        if n in grouped_of:
                            weights[divmod(n, UNITS)] = quantise_weight(*divmod(n, UNITS), grouped_of[n])

        def add_share(k):
            if added_on_gpsimd(k):
                own, other = products_of[k][:, COS:KINDS, :], products_of[k][:, MINUS_SIN:COS, :]
                nc.gpsimd.tensor_tensor(out=own, in0=own, in1=other, op=ALU.add)

        def turn_pair(k, b):
            quad, e = divmod(k, PARITIES)
            if (quad, b) not in sums_of:
                spare = quad == LAST_QUAD and b >= BATCH // 2
                if spare:
                    sums_of[(quad, b)] = mx_psum.tile([P, HALVES, PARITIES, P], F32, name="bank", tag="bank")
                else:
                    sums_of[(quad, b)] = sum_psum.tile([P, HALVES, PARITIES, P], F32, name="sums", tag="sums")
            sums = sums_of[(quad, b)]
            tokens = slice(b * P, (b + 1) * P)
            whole = added_on_gpsimd(k)
            for h in range(HALVES):
                nc.tensor.matmul(
                    out=sums[:, h, e, :], lhsT=products_of[k][:, COS + h, tokens], rhs=ident[:],
                    is_transpose=True, start=True, stop=whole,
                )
                if not whole:
                    nc.tensor.matmul(
                        out=sums[:, h, e, :], lhsT=products_of[k][:, MINUS_SIN + h, tokens], rhs=ident[:],
                        is_transpose=True, start=False, stop=True,
                    )

        def bring_out(quad, b):
            t, z, g, parity = where(PARITIES * quad)
            if (t, z) not in stage_of:
                stage_of[(t, z)] = stage_pool.tile([P, BATCH, D_OUT], F32, name="stage", tag="stage")
            stage = stage_of[(t, z)]
            last_stage = (t, z) == (N_BLOCKS - 1, 1)
            order = "p (g h c) -> p g h c" if last_stage else "p (h g c) -> p g h c"
            by_group = stage[:, b, :].rearrange(order, h=HALVES, g=GROUPS)[:, g]
            nc.scalar.copy(
                out=by_group.rearrange("p h (c e) -> p h c e", e=PARITIES),
                in_=sums_of[(quad, b)][:].rearrange("p h e c -> p h c e"),
            )
            rows = outs[z][b, t * P : (t + 1) * P, :]
            if last_stage:
                nc.sync.dma_start(
                    out=rows.rearrange("p (h g c) -> p g h c", h=HALVES, g=GROUPS)[:, g], in_=by_group
                )
            elif g == GROUPS - 1:
                nc.sync.dma_start(out=rows, in_=stage[:, b, :])

        def turn_half(k):
            quad, part = divmod(k, PARITIES)
            if quad == LAST_QUAD:
                for b in range(BATCH):
                    turn_pair(k, b)
                    if part == 1:
                        bring_out(quad, b)
            else:
                for b in (2 * part, 2 * part + 1):
                    turn_pair(PARITIES * quad, b)
                    turn_pair(PARITIES * quad + 1, b)
                    bring_out(quad, b)

        turn_x(0, 0)
        turn_x(0, 2)
        folds(0, 0)
        sines(0, 0, range(KINDS))
        bias_rows_f32 = const.tile([P, PARITIES * P], F32, name="bias_rows_f32")
        nc.scalar.copy(out=bias_rows_f32[:], in_=bias_rows[:])
        bias_cols = sum_psum.tile([P, PARITIES, P], F32, name="bias_cols", tag="sums")
        for e in range(PARITIES):
            nc.tensor.transpose(out=bias_cols[:, e, :], in_=bias_rows_f32[:, e : 2 * P : 2], identity=ident[:])
        quantise_x(0)
        weights = {}
        weights[(0, 0)] = quantise_weight(0, 0, group_weight(nc.vector, 0, 0))
        bias = const.tile([P, PARITIES, 2 * N_FREQ], F32, name="bias")
        nc.vector.tensor_copy(out=bias[:], in_=bias_cols[:, :, 0 : 2 * N_FREQ])
        project(0)
        grouped_of = {}
        for n in range(1, 2 * UNITS):
            z, u = divmod(n, UNITS)
            grouped_of[n] = group_weight(nc.scalar if n in GROUPED_ON_SCALAR else nc.gpsimd, z, u)
        folds(0, 1)
        sines(0, 1, range(KINDS))

        turned = 0
        for k in range(N_PAIRS + TURN_LAG):
            if 0 < k < N_PAIRS - 1:
                project(k + 1)
            if k + 1 < N_PAIRS:
                multiply_share(k + 1)
            if k < N_PAIRS:
                rotate(k)
                if k == 0:
                    project(1)
                add_share(k)
            lag = TURN_LAG if shared(turned) else TURN_LAG - 1
            if turned < N_PAIRS and turned + lag <= k:
                turn_half(turned)
                turned += 1
            t, part = divmod(k, PAIRS_PER_BLOCK)
            if t + 1 < N_BLOCKS:
                prepare(t + 1, part)
